import numpy as np
import ml_dtypes


def mxq(x, axis, fmt="e4m3"):
    dtype, down = {"e4m3": (ml_dtypes.float8_e4m3fn, 7), "e5m2": (ml_dtypes.float8_e5m2, 14)}[fmt]
    v = np.moveaxis(np.asarray(x, np.float32).astype(ml_dtypes.bfloat16).astype(np.float64), axis, -1)
    blocks = v.reshape(v.shape[:-1] + (-1, 32))
    amax = np.abs(blocks).max(-1, keepdims=True)
    byte = np.maximum(np.where(amax > 0, np.frexp(amax)[1] - 1 + 127, 0) - down, 1)
    scale = np.exp2(byte - 127.0)
    codes = (blocks / scale).astype(np.float32).astype(dtype).astype(np.float64)
    return np.moveaxis((codes * scale).reshape(v.shape), -1, axis)


WIDE = False


def mx_kscale(k):
    if not WIDE:
        return np.ones(k)
    levels = np.array([10, -10, 5, -5, 0])
    a = np.random.permutation(np.resize(levels, k // 512 * 4)).reshape(k // 512, 4)
    idx = np.arange(k)
    return np.exp2(a[idx // 512, idx % 128 // 32])


BF16 = ml_dtypes.bfloat16


def bf(x):
    return np.asarray(x, np.float32).astype(BF16)


def f64(x):
    return np.asarray(x).astype(np.float64)


B, T, HIDDEN, NUM_HEADS, HEAD_DIM, ROT_DIM, LATENT = 2, 512, 2048, 16, 128, 64, 512
NOPE_DIM = HEAD_DIM - ROT_DIM
BASE = 10000.0


def rope_tables():
    inv_freq = 1.0 / (BASE ** (np.arange(0, ROT_DIM, 2) / ROT_DIM))
    freqs = np.arange(T)[:, None] * inv_freq[None, :]
    emb = np.concatenate((freqs, freqs), axis=-1)
    return np.cos(emb), np.sin(emb)


def rotate_half(v):
    v1, v2 = v[..., : v.shape[-1] // 2], v[..., v.shape[-1] // 2 :]
    return np.concatenate((-v2, v1), axis=-1)


def heads(y, d):
    return y.reshape(B, T, NUM_HEADS, d).transpose(0, 2, 1, 3)


def setup_inputs():
    s, t = mx_kscale(HIDDEN), mx_kscale(LATENT)
    cos, sin = rope_tables()
    return {"x": bf(np.random.standard_normal((B, T, HIDDEN)) * s),
            "Wkv_d": bf(np.random.standard_normal((HIDDEN, LATENT)) / np.sqrt(HIDDEN) / s[:, None] * t),
            "Wk_nope": bf(np.random.standard_normal((LATENT, NUM_HEADS * NOPE_DIM)) / np.sqrt(LATENT) / t[:, None]),
            "Wv_u": bf(np.random.standard_normal((LATENT, NUM_HEADS * HEAD_DIM)) / np.sqrt(LATENT) / t[:, None]),
            "Wrk": bf(np.random.standard_normal((HIDDEN, NUM_HEADS * ROT_DIM)) / np.sqrt(HIDDEN) / s[:, None]),
            "cos": bf(cos), "sin": bf(sin)}


def reference(x, Wkv_d, Wk_nope, Wv_u, Wrk, cos, sin):
    xq = mxq(f64(x), 2, "e4m3")
    kv_latent = xq @ mxq(f64(Wkv_d), 0, "e4m3")
    lq = mxq(kv_latent, 2, "e4m3")
    k_nope = heads(lq @ mxq(f64(Wk_nope), 0, "e4m3"), NOPE_DIM)
    v = heads(lq @ mxq(f64(Wv_u), 0, "e4m3"), HEAD_DIM)
    k_rot = heads(xq @ mxq(f64(Wrk), 0, "e4m3"), ROT_DIM)
    c, sn = f64(cos)[None, None, :, :], f64(sin)[None, None, :, :]
    k_rot = k_rot * c + rotate_half(k_rot) * sn
    k = np.concatenate([k_rot, k_nope], axis=-1)
    return k, v

@@ -1,0 +1,239 @@
+from contextlib import ExitStack
+
+import concourse.mybir as mybir
+from concourse.masks import make_identity
+
+BF16 = mybir.dt.bfloat16
+F32 = mybir.dt.float32
+U32 = mybir.dt.uint32
+U8 = mybir.dt.uint8
+FP8X4 = mybir.dt.float8_e4m3fn_x4
+MULT = mybir.AluOpType.mult
+ADD = mybir.AluOpType.add
+
+P = 128
+FLOPS = 2 * 1024 * (2048 * 512 + 2048 * 1024 + 512 * 1024 + 512 * 2048)
+
+SCALAR_UNITS = ("kv1", "kv3", "v1", "v3", "r01", "r11", "r21")
+
+
+def tile_multiheadlatentattention_pb_kernel(
+    tc, x, Wkv_d, Wk_nope, Wv_u, Wrk, cos, sin, out_0, out_1
+):
+    nc = tc.nc
+    with ExitStack() as ctx:
+        const = ctx.enter_context(tc.tile_pool(name="const", bufs=1))
+        big = ctx.enter_context(tc.tile_pool(name="big", bufs=13))
+        grp = ctx.enter_context(tc.tile_pool(name="grp", bufs=6))
+        keep = ctx.enter_context(tc.tile_pool(name="keep", bufs=1))
+        tmpp = ctx.enter_context(tc.tile_pool(name="tmpp", bufs=2))
+        psum = ctx.enter_context(tc.psum_pool(name="psum", bufs=8))
+
+        ident = const.tile([P, P], F32, name="ident")
+        make_identity(nc, ident[:])
+        cos_b = const.tile([P, 4, 64], BF16, name="cos_b")
+        sin_b = const.tile([P, 4, 64], BF16, name="sin_b")
+        nc.scalar.dma_start(out=cos_b[:], in_=cos.rearrange("(p j) d -> p j d", j=4))
+        nc.scalar.dma_start(out=sin_b[:], in_=sin.rearrange("(p j) d -> p j d", j=4))
+
+        def load(view, label):
+            raw = big.tile([P, 4096], BF16, tag="big", name="raw_" + label)
+            nc.sync.dma_start(
+                out=raw[:].rearrange("p (a f) -> p a f", a=view.shape[1]), in_=view
+            )
+            return raw
+
+        def load_x(b):
+            xv = x[b].rearrange("(p j) k -> p j k", j=4)
+            return [load(xv[:, 2 * a : 2 * a + 2, :], "x%d%d" % (b, a)) for a in range(2)]
+
+        x_raw = {}
+        x_raw[0] = load_x(0)
+        kv_raw = [
+            load(
+                Wkv_d[1024 * a : 1024 * a + 1024, :].rearrange(
+                    "(g u p e) n -> p (g u) (e n)", g=2, u=2, p=P, e=2
+                ),
+                "kv%d" % a,
+            )
+            for a in range(2)
+        ]
+        wv_view = Wv_u.rearrange("(t p) n -> p t n", t=4)
+        v_raw = [load(wv_view[:, :, 1024 * a : 1024 * a + 1024], "v%d" % a) for a in range(2)]
+        x_raw[1] = load_x(1)
+        n_raw = load(Wk_nope.rearrange("(t p) n -> p t n", t=4), "n")
+        r_raw = [
+            load(
+                Wrk[512 * g : 512 * g + 512, :].rearrange(
+                    "(u p e) n -> p u (e n)", u=2, p=P, e=2
+                ),
+                "r%d" % g,
+            )
+            for g in range(4)
+        ]
+
+        cosf = const.tile([P, 4, 64], F32, name="cosf")
+        sinsw = const.tile([P, 4, 64], F32, name="sinsw")
+        nc.vector.tensor_copy(out=cosf[:], in_=cos_b[:])
+        nc.vector.tensor_copy(out=sinsw[:, :, 0:32], in_=sin_b[:, :, 32:64])
+        nc.vector.tensor_scalar_mul(out=sinsw[:, :, 32:64], in0=sin_b[:, :, 0:32], scalar1=-1.0)
+
+        def quantise(grouped, label):
+            codes = keep.tile([P, 512], U32, name="c_" + label, align_bytes=64)
+            scales = keep.tile([P, 512], U8, name="s_" + label, align_bytes=64)
+            nc.vector.quantize_mx(
+                out=codes[:].bitcast(FP8X4), scales=scales[:], in_=grouped[:]
+            )
+            return (codes, scales)
+
+        def weight_unit(src, label):
+            grouped = grp.tile([P, 2048], BF16, tag="g", name="g_" + label, align_bytes=64)
+            dst = grouped[:].rearrange("p (c i t) -> p c t i", i=4, t=4)
+            s = src.rearrange("p t (c i) -> p c t i", i=4)
+            if label in SCALAR_UNITS:
+                nc.scalar.copy(out=dst, in_=s)
+            else:
+                nc.vector.tensor_copy(out=dst, in_=s)
+            return quantise(grouped, label)
+
+        def mx(out, a, acols, b, bcols, start, stop):
+            nc.tensor.matmul_mx(
+                out=out,
+                lhsT=a[0][:, acols].bitcast(FP8X4),
+                lhsT_scale=a[1][:, acols],
+                rhs=b[0][:, bcols].bitcast(FP8X4),
+                rhs_scale=b[1][:, bcols],
+                start=start,
+                stop=stop,
+            )
+
+        def cols(i, w):
+            return slice(i * w, i * w + w)
+
+        xq = {}
+        lq = {}
+
+        def x_tiles(b):
+            for j in range(4):
+                xw = x_raw[b][j // 2][:].bitcast(F32)
+                grouped = grp.tile([P, 2048], BF16, tag="g", name="g_x", align_bytes=64)
+                gw = grouped[:].bitcast(F32).rearrange("p (g r u) -> p g r u", g=4, u=2)
+                for gp in range(2):
+                    xt = psum.tile([P, 512], F32, tag="ps", name="xt")
+                    xt3 = xt[:].rearrange("p (a r) -> p a r", a=4)
+                    for a in range(4):
+                        c0 = 1024 * (j % 2) + 512 * gp + 128 * a
+                        nc.tensor.transpose(xt3[:, a, :], xw[:, c0 : c0 + 128], ident[:])
+                    nc.scalar.copy(
+                        out=gw[:, 2 * gp : 2 * gp + 2, :, :],
+                        in_=xt[:].rearrange("p (g u r) -> p g r u", g=2, u=2),
+                    )
+                xq[4 * b + j] = quantise(grouped, "x%d" % (4 * b + j))
+
+        def latent(b):
+            grouped = grp.tile([P, 2048], BF16, tag="g", name="g_l", align_bytes=64)
+            g4 = grouped[:].rearrange("p (j r t) -> p j r t", j=4, t=4)
+            for j in range(4):
+                pl = psum.tile([P, 512], F32, tag="ps", name="pl")
+                pl3 = pl[:].rearrange("p (t r) -> p t r", t=4)
+                for t in range(4):
+                    for g in range(4):
+                        mx(pl3[:, t, :], kvq[g], cols(t, 128), xq[4 * b + j], cols(g, 128), g == 0, g == 3)
+                nc.scalar.copy(out=g4[:, j, :, :], in_=pl[:].rearrange("p (t r) -> p r t", t=4))
+            lq[b] = quantise(grouped, "l%d" % b)
+
+        def v_chunk(b, hc):
+            vsb = big.tile([P, 2048], F32, tag="big", name="vsb")
+            v4 = vsb[:].rearrange("p (h j d) -> p h j d", h=4, j=4)
+            for j in range(4):
+                pv = psum.tile([P, 512], F32, tag="ps", name="pv")
+                mx(pv[:], lq[b], cols(j, 128), vq[hc], cols(0, 512), True, True)
+                nc.scalar.copy(out=v4[:, :, j, :], in_=pv[:].rearrange("p (h d) -> p h d", h=4))
+            nc.sync.dma_start(
+                out=out_1[b, 4 * hc : 4 * hc + 4].rearrange("h (p j) d -> p h (j d)", j=4),
+                in_=vsb[:].rearrange("p (h f) -> p h f", h=4),
+            )
+
+        def k_chunk(b, hc):
+            ksb = big.tile([P, 2048], F32, tag="big", name="ksb")
+            k4 = ksb[:].rearrange("p (h j d) -> p h j d", h=4, j=4)
+            tmp = tmpp.tile([P, 1024], F32, tag="tmp", name="tmp")
+            t4 = tmp[:].rearrange("p (h j d) -> p h j d", h=4, j=4)
+            half = hc // 2
+            wc = cols(hc % 2, 256)
+            for jp in range(2):
+                js = slice(2 * jp, 2 * jp + 2)
+                pr = psum.tile([P, 512], F32, tag="ps", name="pr")
+                pr3 = pr[:].rearrange("p (j n) -> p j n", j=2)
+                for jj in range(2):
+                    for g in range(4):
+                        mx(pr3[:, jj, :], xq[4 * b + 2 * jp + jj], cols(g, 128), rq[(g, half)], wc, g == 0, g == 3)
+                pn = psum.tile([P, 512], F32, tag="ps", name="pn")
+                pn3 = pn[:].rearrange("p (j n) -> p j n", j=2)
+                for jj in range(2):
+                    mx(pn3[:, jj, :], lq[b], cols(2 * jp + jj, 128), nq[half], wc, True, True)
+                r4 = pr[:].rearrange("p (j h d) -> p j h d", j=2, h=4)
+                nc.vector.tensor_tensor(
+                    out=k4[:, :, js, 0:64].rearrange("p h j d -> p j h d"),
+                    in0=r4,
+                    in1=cosf[:, js, :].unsqueeze(2).to_broadcast([P, 2, 4, 64]),
+                    op=MULT,
+                )
+                nc.vector.tensor_tensor(
+                    out=t4[:, :, js, :].rearrange("p h j d -> p j h d"),
+                    in0=r4,
+                    in1=sinsw[:, js, :].unsqueeze(2).to_broadcast([P, 2, 4, 64]),
+                    op=MULT,
+                )
+                nc.scalar.copy(
+                    out=k4[:, :, js, 64:128].rearrange("p h j d -> p j h d"),
+                    in_=pn[:].rearrange("p (j h d) -> p j h d", j=2, h=4),
+                )
+            for s in range(2):
+                nc.vector.tensor_tensor(
+                    out=k4[:, :, :, 32 * s : 32 * s + 32],
+                    in0=k4[:, :, :, 32 * s : 32 * s + 32],
+                    in1=t4[:, :, :, 32 - 32 * s : 64 - 32 * s],
+                    op=ADD,
+                )
+            nc.sync.dma_start(
+                out=out_0[b, 4 * hc : 4 * hc + 4].rearrange("h (p j) d -> p h (j d)", j=4),
+                in_=ksb[:].rearrange("p (h f) -> p h f", h=4),
+            )
+
+        x_tiles(0)
+        kvq = [
+            weight_unit(
+                kv_raw[g // 2][:].rearrange("p (g t n) -> p g t n", g=2, t=4)[:, g % 2, :, :],
+                "kv%d" % g,
+            )
+            for g in range(4)
+        ]
+        latent(0)
+        vq = [
+            weight_unit(
+                v_raw[hc // 2][:].rearrange("p (t n) -> p t n", t=4)[:, :, cols(hc % 2, 512)],
+                "v%d" % hc,
+            )
+            for hc in range(4)
+        ]
+        for hc in range(4):
+            v_chunk(0, hc)
+        x_tiles(1)
+        latent(1)
+        nq = [
+            weight_unit(n_raw[:].rearrange("p (t n) -> p t n", t=4)[:, :, cols(h, 512)], "n%d" % h)
+            for h in range(2)
+        ]
+        rq = {}
+        for g in range(4):
+            for h in range(2):
+                rq[(g, h)] = weight_unit(
+                    r_raw[g][:].rearrange("p (t n) -> p t n", t=4)[:, :, cols(h, 512)],
+                    "r%d%d" % (g, h),
+                )
+        for hc in range(4):
+            k_chunk(0, hc)
+            v_chunk(1, hc)
+        for hc in range(4):
+            k_chunk(1, hc)

@@ -14,7 +14,39 @@ ADD = mybir.AluOpType.add
 P = 128
 FLOPS = 2 * 1024 * (2048 * 512 + 2048 * 1024 + 512 * 1024 + 512 * 2048)
 
-SCALAR_UNITS = ("kv1", "kv3", "v1", "v3", "r01", "r11", "r21")
+ON_VECTOR = (
+    "xc40", "nc000", "nc021",
+)
+ON_SCALAR = (
+    "WUv2", "WUv3",
+)
+ORDER = (
+    "Lx0", "Lx1", "T00", "T01", "xc00", "T10", "Lkv0", "T11", "xc01", "xc10", "XQ0", "xc11", "T20",
+    "T21", "xc20", "XQ1", "T30", "Lkv1", "T31", "xc21", "xc30", "XQ2", "xc31", "WUkv0", "Lx2",
+    "WUkv1", "XQ3", "WUkv2", "Lx3", "WUkv3", "T40", "T41", "WQkv0", "T50", "Lv0", "xc41", "T51",
+    "WQkv1", "xc50", "WQkv2", "xc51", "T60", "WQkv3", "T61", "xc60", "T70", "xc40", "Lr0", "LT0",
+    "xc61", "XQ5", "xc70", "XQ4", "LT1", "lc0", "WUv0", "Lr1", "LT2", "lc1", "WUv1", "LT3", "WQv0",
+    "lc2", "XQ6", "Lr2", "T71", "WQv1", "lc3", "LT4", "WUr00", "xc71", "LT5", "lc4", "LQ0", "Lr3",
+    "XQ7", "v000", "lc5", "WUr10", "v001", "v002", "vc000", "v003", "LT6", "vc001", "WUr20", "Ln0",
+    "vc002", "LT7", "vc003", "WQr00", "lc6", "WUr30", "v010", "lc7", "Lv1", "v011", "v012",
+    "WQr10", "vc010", "v013", "LQ1", "vc011", "WQr20", "vc012", "v100", "v101", "WQr30", "vc013",
+    "v102", "Sv00", "v103", "vc100", "WUn0", "v110", "v111", "vc101", "v112", "v113", "vc102",
+    "WUr01", "r000", "vc103", "Sv01", "vc110", "WQn0", "r001", "vc111", "m1000", "vc112", "m2000",
+    "n000", "n001", "vc113", "m1001", "r100", "nc001", "m2001", "Sv10", "WUv2", "r101", "nc000",
+    "a000", "m1100", "n100", "m2100", "a100", "n101", "r010", "m1101", "Sv11", "nc100", "m2101",
+    "nc101", "r011", "WQv2", "a010", "WUv3", "m1010", "v020", "m2010", "v021", "a110", "Sk00",
+    "v022", "m1011", "v023", "n010", "m2011", "n011", "vc020", "v120", "WUr11", "v121", "a001",
+    "vc021", "v122", "v123", "vc022", "Sk10", "WUr21", "r110", "vc023", "a101", "nc010", "WUr31",
+    "r111", "nc011", "vc120", "m1110", "Sv02", "n110", "vc121", "n111", "m2110", "vc122", "m1111",
+    "vc123", "m2111", "nc110", "WQv3", "nc111", "a011", "Sk01", "WQr01", "v030", "v031", "WQr11",
+    "vc030", "a111", "v032", "v033", "WQr21", "vc031", "v130", "v131", "vc032", "WQr31", "v132",
+    "Sv12", "v133", "vc033", "WUn1", "r020", "vc130", "vc131", "WQn1", "r021", "vc132", "m1020",
+    "Sk11", "vc133", "m2020", "n020", "n021", "nc020", "m1021", "r120", "m2021", "r121", "nc021",
+    "a002", "Sv03", "m1120", "n120", "m2120", "a102", "n121", "nc120", "r030", "m1121", "nc121",
+    "m2121", "r031", "Sk02", "m1030", "a012", "m2030", "n030", "m1031", "n031", "a112", "nc030",
+    "r130", "m2031", "nc031", "Sv13", "a003", "r131", "m1130", "m2130", "a103", "n130", "m1131",
+    "n131", "nc130", "m2131", "nc131", "Sk12", "a013", "a113", "Sk03", "Sk13",
+)
 
 
 def tile_multiheadlatentattention_pb_kernel(
@@ -28,6 +60,7 @@ def tile_multiheadlatentattention_pb_kernel(
         keep = ctx.enter_context(tc.tile_pool(name="keep", bufs=1))
         tmpp = ctx.enter_context(tc.tile_pool(name="tmpp", bufs=2))
         psum = ctx.enter_context(tc.psum_pool(name="psum", bufs=8))
+        ctx.enter_context(tc.manual_schedule())
 
         ident = const.tile([P, P], F32, name="ident")
         make_identity(nc, ident[:])
@@ -35,205 +68,286 @@ def tile_multiheadlatentattention_pb_kernel(
         sin_b = const.tile([P, 4, 64], BF16, name="sin_b")
         nc.scalar.dma_start(out=cos_b[:], in_=cos.rearrange("(p j) d -> p j d", j=4))
         nc.scalar.dma_start(out=sin_b[:], in_=sin.rearrange("(p j) d -> p j d", j=4))
-
-        def load(view, label):
-            raw = big.tile([P, 4096], BF16, tag="big", name="raw_" + label)
-            nc.sync.dma_start(
-                out=raw[:].rearrange("p (a f) -> p a f", a=view.shape[1]), in_=view
-            )
-            return raw
-
-        def load_x(b):
-            xv = x[b].rearrange("(p j) k -> p j k", j=4)
-            return [load(xv[:, 2 * a : 2 * a + 2, :], "x%d%d" % (b, a)) for a in range(2)]
-
-        x_raw = {}
-        x_raw[0] = load_x(0)
-        kv_raw = [
-            load(
-                Wkv_d[1024 * a : 1024 * a + 1024, :].rearrange(
-                    "(g u p e) n -> p (g u) (e n)", g=2, u=2, p=P, e=2
-                ),
-                "kv%d" % a,
-            )
-            for a in range(2)
-        ]
-        wv_view = Wv_u.rearrange("(t p) n -> p t n", t=4)
-        v_raw = [load(wv_view[:, :, 1024 * a : 1024 * a + 1024], "v%d" % a) for a in range(2)]
-        x_raw[1] = load_x(1)
-        n_raw = load(Wk_nope.rearrange("(t p) n -> p t n", t=4), "n")
-        r_raw = [
-            load(
-                Wrk[512 * g : 512 * g + 512, :].rearrange(
-                    "(u p e) n -> p u (e n)", u=2, p=P, e=2
-                ),
-                "r%d" % g,
-            )
-            for g in range(4)
-        ]
-
         cosf = const.tile([P, 4, 64], F32, name="cosf")
         sinsw = const.tile([P, 4, 64], F32, name="sinsw")
         nc.vector.tensor_copy(out=cosf[:], in_=cos_b[:])
         nc.vector.tensor_copy(out=sinsw[:, :, 0:32], in_=sin_b[:, :, 32:64])
         nc.vector.tensor_scalar_mul(out=sinsw[:, :, 32:64], in0=sin_b[:, :, 0:32], scalar1=-1.0)
 
-        def quantise(grouped, label):
-            codes = keep.tile([P, 512], U32, name="c_" + label, align_bytes=64)
-            scales = keep.tile([P, 512], U8, name="s_" + label, align_bytes=64)
-            nc.vector.quantize_mx(
-                out=codes[:].bitcast(FP8X4), scales=scales[:], in_=grouped[:]
-            )
-            return (codes, scales)
-
-        def weight_unit(src, label):
-            grouped = grp.tile([P, 2048], BF16, tag="g", name="g_" + label, align_bytes=64)
-            dst = grouped[:].rearrange("p (c i t) -> p c t i", i=4, t=4)
-            s = src.rearrange("p t (c i) -> p c t i", i=4)
-            if label in SCALAR_UNITS:
-                nc.scalar.copy(out=dst, in_=s)
-            else:
-                nc.vector.tensor_copy(out=dst, in_=s)
-            return quantise(grouped, label)
-
-        def mx(out, a, acols, b, bcols, start, stop):
-            nc.tensor.matmul_mx(
-                out=out,
-                lhsT=a[0][:, acols].bitcast(FP8X4),
-                lhsT_scale=a[1][:, acols],
-                rhs=b[0][:, bcols].bitcast(FP8X4),
-                rhs_scale=b[1][:, bcols],
-                start=start,
-                stop=stop,
-            )
+        tiles = {}
+        ops = {}
 
         def cols(i, w):
             return slice(i * w, i * w + w)
 
-        xq = {}
-        lq = {}
+        def big_tile(key, dtype, width):
+            if key not in tiles:
+                tiles[key] = big.tile([P, width], dtype, tag="big", name=key)
+            return tiles[key]
 
-        def x_tiles(b):
-            for j in range(4):
-                xw = x_raw[b][j // 2][:].bitcast(F32)
-                grouped = grp.tile([P, 2048], BF16, tag="g", name="g_x", align_bytes=64)
-                gw = grouped[:].bitcast(F32).rearrange("p (g r u) -> p g r u", g=4, u=2)
-                for gp in range(2):
-                    xt = psum.tile([P, 512], F32, tag="ps", name="xt")
-                    xt3 = xt[:].rearrange("p (a r) -> p a r", a=4)
-                    for a in range(4):
-                        c0 = 1024 * (j % 2) + 512 * gp + 128 * a
-                        nc.tensor.transpose(xt3[:, a, :], xw[:, c0 : c0 + 128], ident[:])
-                    nc.scalar.copy(
-                        out=gw[:, 2 * gp : 2 * gp + 2, :, :],
-                        in_=xt[:].rearrange("p (g u r) -> p g r u", g=2, u=2),
-                    )
-                xq[4 * b + j] = quantise(grouped, "x%d" % (4 * b + j))
+        def grp_tile(key):
+            if key not in tiles:
+                tiles[key] = grp.tile([P, 2048], BF16, tag="g", name=key, align_bytes=64)
+            return tiles[key]
 
-        def latent(b):
-            grouped = grp.tile([P, 2048], BF16, tag="g", name="g_l", align_bytes=64)
-            g4 = grouped[:].rearrange("p (j r t) -> p j r t", j=4, t=4)
-            for j in range(4):
-                pl = psum.tile([P, 512], F32, tag="ps", name="pl")
-                pl3 = pl[:].rearrange("p (t r) -> p t r", t=4)
-                for t in range(4):
-                    for g in range(4):
-                        mx(pl3[:, t, :], kvq[g], cols(t, 128), xq[4 * b + j], cols(g, 128), g == 0, g == 3)
-                nc.scalar.copy(out=g4[:, j, :, :], in_=pl[:].rearrange("p (t r) -> p r t", t=4))
-            lq[b] = quantise(grouped, "l%d" % b)
+        def ps_tile(key):
+            if key not in tiles:
+                tiles[key] = psum.tile([P, 512], F32, tag="ps", name=key)
+            return tiles[key]
 
-        def v_chunk(b, hc):
-            vsb = big.tile([P, 2048], F32, tag="big", name="vsb")
-            v4 = vsb[:].rearrange("p (h j d) -> p h j d", h=4, j=4)
-            for j in range(4):
-                pv = psum.tile([P, 512], F32, tag="ps", name="pv")
-                mx(pv[:], lq[b], cols(j, 128), vq[hc], cols(0, 512), True, True)
-                nc.scalar.copy(out=v4[:, :, j, :], in_=pv[:].rearrange("p (h d) -> p h d", h=4))
-            nc.sync.dma_start(
-                out=out_1[b, 4 * hc : 4 * hc + 4].rearrange("h (p j) d -> p h (j d)", j=4),
-                in_=vsb[:].rearrange("p (h f) -> p h f", h=4),
+        def copy(name, out, in_):
+            if name in ON_VECTOR:
+                nc.vector.tensor_copy(out=out, in_=in_)
+            else:
+                nc.scalar.copy(out=out, in_=in_)
+
+        def quantise(gkey, label):
+            codes = keep.tile([P, 512], U32, name="c_" + label, align_bytes=64)
+            scales = keep.tile([P, 512], U8, name="s_" + label, align_bytes=64)
+            nc.vector.quantize_mx(
+                out=codes[:].bitcast(FP8X4), scales=scales[:], in_=tiles[gkey][:]
+            )
+            tiles["q" + label] = (codes, scales)
+
+        def mx(out, a, acols, b, bcols, start, stop):
+            qa = tiles["q" + a]
+            qb = tiles["q" + b]
+            nc.tensor.matmul_mx(
+                out=out,
+                lhsT=qa[0][:, acols].bitcast(FP8X4),
+                lhsT_scale=qa[1][:, acols],
+                rhs=qb[0][:, bcols].bitcast(FP8X4),
+                rhs_scale=qb[1][:, bcols],
+                start=start,
+                stop=stop,
             )
 
-        def k_chunk(b, hc):
-            ksb = big.tile([P, 2048], F32, tag="big", name="ksb")
-            k4 = ksb[:].rearrange("p (h j d) -> p h j d", h=4, j=4)
-            tmp = tmpp.tile([P, 1024], F32, tag="tmp", name="tmp")
-            t4 = tmp[:].rearrange("p (h j d) -> p h j d", h=4, j=4)
-            half = hc // 2
-            wc = cols(hc % 2, 256)
-            for jp in range(2):
-                js = slice(2 * jp, 2 * jp + 2)
-                pr = psum.tile([P, 512], F32, tag="ps", name="pr")
-                pr3 = pr[:].rearrange("p (j n) -> p j n", j=2)
+        views = {}
+        for c in range(4):
+            views["x%d" % c] = x[c // 2].rearrange("(p j) k -> p j k", j=4)[
+                :, 2 * (c % 2) : 2 * (c % 2) + 2, :
+            ]
+            views["r%d" % c] = Wrk[512 * c : 512 * c + 512, :].rearrange(
+                "(u p e) n -> p u (e n)", u=2, p=P, e=2
+            )
+        for c in range(2):
+            views["kv%d" % c] = Wkv_d[1024 * c : 1024 * c + 1024, :].rearrange(
+                "(g u p e) n -> p (g u) (e n)", g=2, u=2, p=P, e=2
+            )
+            views["v%d" % c] = Wv_u.rearrange("(t p) n -> p t n", t=4)[
+                :, :, 1024 * c : 1024 * c + 1024
+            ]
+        views["n0"] = Wk_nope.rearrange("(t p) n -> p t n", t=4)
+
+        def make_load(label):
+            def run():
+                view = views[label]
+                raw = big_tile("raw" + label, BF16, 4096)
+                nc.sync.dma_start(
+                    out=raw[:].rearrange("p (a f) -> p a f", a=view.shape[1]), in_=view
+                )
+
+            return run
+
+        for label in views:
+            ops["L" + label] = make_load(label)
+
+        def make_t(i, h):
+            def run():
+                xw = tiles["rawx%d" % (i // 2)][:].bitcast(F32)
+                xt3 = ps_tile("px%d%d" % (i, h))[:].rearrange("p (a r) -> p a r", a=4)
+                for a in range(4):
+                    c0 = 1024 * (i % 2) + 512 * h + 128 * a
+                    nc.tensor.transpose(xt3[:, a, :], xw[:, c0 : c0 + 128], ident[:])
+
+            return run
+
+        def make_xc(i, h):
+            def run():
+                gw = grp_tile("gx%d" % i)[:].bitcast(F32).rearrange("p (g r u) -> p g r u", g=4, u=2)
+                copy(
+                    "xc%d%d" % (i, h),
+                    gw[:, 2 * h : 2 * h + 2, :, :],
+                    tiles["px%d%d" % (i, h)][:].rearrange("p (g u r) -> p g r u", g=2, u=2),
+                )
+
+            return run
+
+        def make_q(gkey, label):
+            def run():
+                quantise(gkey, label)
+
+            return run
+
+        for i in range(8):
+            for h in range(2):
+                ops["T%d%d" % (i, h)] = make_t(i, h)
+                ops["xc%d%d" % (i, h)] = make_xc(i, h)
+            ops["XQ%d" % i] = make_q("gx%d" % i, "x%d" % i)
+
+        def make_wu(label, rawkey, pick):
+            def run():
+                src = pick(tiles[rawkey][:])
+                dst = grp_tile("g" + label)[:].rearrange("p (c i t) -> p c t i", i=4, t=4)
+                s = src.rearrange("p t (c i) -> p c t i", i=4)
+                if ("WU" + label) in ON_SCALAR:
+                    nc.scalar.copy(out=dst, in_=s)
+                else:
+                    nc.vector.tensor_copy(out=dst, in_=s)
+
+            return run
+
+        def pick_kv(g):
+            return lambda ap: ap.rearrange("p (g t n) -> p g t n", g=2, t=4)[:, g, :, :]
+
+        def pick_half(h):
+            return lambda ap: ap.rearrange("p (t n) -> p t n", t=4)[:, :, cols(h, 512)]
+
+        units = []
+        for g in range(4):
+            units.append(("kv%d" % g, "rawkv%d" % (g // 2), pick_kv(g % 2)))
+            units.append(("v%d" % g, "rawv%d" % (g // 2), pick_half(g % 2)))
+            for h in range(2):
+                units.append(("r%d%d" % (g, h), "rawr%d" % g, pick_half(h)))
+        for h in range(2):
+            units.append(("n%d" % h, "rawn0", pick_half(h)))
+        for label, rawkey, pick in units:
+            ops["WU" + label] = make_wu(label, rawkey, pick)
+            ops["WQ" + label] = make_q("g" + label, label)
+
+        def make_lt(i):
+            def run():
+                pl3 = ps_tile("pl%d" % i)[:].rearrange("p (t r) -> p t r", t=4)
+                for t in range(4):
+                    for g in range(4):
+                        mx(pl3[:, t, :], "kv%d" % g, cols(t, 128), "x%d" % i, cols(g, 128), g == 0, g == 3)
+
+            return run
+
+        def make_lc(i):
+            def run():
+                g4 = grp_tile("gl%d" % (i // 4))[:].rearrange("p (j r t) -> p j r t", j=4, t=4)
+                copy("lc%d" % i, g4[:, i % 4, :, :], tiles["pl%d" % i][:].rearrange("p (t r) -> p r t", t=4))
+
+            return run
+
+        for i in range(8):
+            ops["LT%d" % i] = make_lt(i)
+            ops["lc%d" % i] = make_lc(i)
+        for b in range(2):
+            ops["LQ%d" % b] = make_q("gl%d" % b, "l%d" % b)
+
+        def make_v(b, hc, j):
+            def run():
+                mx(ps_tile("pv%d%d%d" % (b, hc, j))[:], "l%d" % b, cols(j, 128), "v%d" % hc, cols(0, 512), True, True)
+
+            return run
+
+        def make_vc(b, hc, j):
+            def run():
+                v4 = big_tile("vs%d%d" % (b, hc), F32, 2048)[:].rearrange("p (h j d) -> p h j d", h=4, j=4)
+                copy(
+                    "vc%d%d%d" % (b, hc, j),
+                    v4[:, :, j, :],
+                    tiles["pv%d%d%d" % (b, hc, j)][:].rearrange("p (h d) -> p h d", h=4),
+                )
+
+            return run
+
+        def make_store(dram, key, b, hc):
+            def run():
+                nc.sync.dma_start(
+                    out=dram[b, 4 * hc : 4 * hc + 4].rearrange("h (p j) d -> p h (j d)", j=4),
+                    in_=tiles[key][:].rearrange("p (h f) -> p h f", h=4),
+                )
+
+            return run
+
+        def k_view(b, hc):
+            return big_tile("ks%d%d" % (b, hc), F32, 2048)[:].rearrange("p (h j d) -> p h j d", h=4, j=4)
+
+        def t_view(b, hc):
+            key = "tm%d%d" % (b, hc)
+            if key not in tiles:
+                tiles[key] = tmpp.tile([P, 1024], F32, tag="tmp", name=key)
+            return tiles[key][:].rearrange("p (h j d) -> p h j d", h=4, j=4)
+
+        def make_r(b, hc, jp):
+            def run():
+                pr3 = ps_tile("pr%d%d%d" % (b, hc, jp))[:].rearrange("p (j n) -> p j n", j=2)
                 for jj in range(2):
                     for g in range(4):
-                        mx(pr3[:, jj, :], xq[4 * b + 2 * jp + jj], cols(g, 128), rq[(g, half)], wc, g == 0, g == 3)
-                pn = psum.tile([P, 512], F32, tag="ps", name="pn")
-                pn3 = pn[:].rearrange("p (j n) -> p j n", j=2)
+                        mx(pr3[:, jj, :], "x%d" % (4 * b + 2 * jp + jj), cols(g, 128), "r%d%d" % (g, hc // 2), cols(hc % 2, 256), g == 0, g == 3)
+
+            return run
+
+        def make_n(b, hc, jp):
+            def run():
+                pn3 = ps_tile("pn%d%d%d" % (b, hc, jp))[:].rearrange("p (j n) -> p j n", j=2)
                 for jj in range(2):
-                    mx(pn3[:, jj, :], lq[b], cols(2 * jp + jj, 128), nq[half], wc, True, True)
-                r4 = pr[:].rearrange("p (j h d) -> p j h d", j=2, h=4)
+                    mx(pn3[:, jj, :], "l%d" % b, cols(2 * jp + jj, 128), "n%d" % (hc // 2), cols(hc % 2, 256), True, True)
+
+            return run
+
+        def make_m(which, b, hc, jp):
+            def run():
+                js = slice(2 * jp, 2 * jp + 2)
+                r4 = tiles["pr%d%d%d" % (b, hc, jp)][:].rearrange("p (j h d) -> p j h d", j=2, h=4)
+                if which == 1:
+                    out = k_view(b, hc)[:, :, js, 0:64]
+                    table = cosf
+                else:
+                    out = t_view(b, hc)[:, :, js, :]
+                    table = sinsw
                 nc.vector.tensor_tensor(
-                    out=k4[:, :, js, 0:64].rearrange("p h j d -> p j h d"),
+                    out=out.rearrange("p h j d -> p j h d"),
                     in0=r4,
-                    in1=cosf[:, js, :].unsqueeze(2).to_broadcast([P, 2, 4, 64]),
+                    in1=table[:, js, :].unsqueeze(2).to_broadcast([P, 2, 4, 64]),
                     op=MULT,
                 )
-                nc.vector.tensor_tensor(
-                    out=t4[:, :, js, :].rearrange("p h j d -> p j h d"),
-                    in0=r4,
-                    in1=sinsw[:, js, :].unsqueeze(2).to_broadcast([P, 2, 4, 64]),
-                    op=MULT,
+
+            return run
+
+        def make_nc(b, hc, jp):
+            def run():
+                js = slice(2 * jp, 2 * jp + 2)
+                copy(
+                    "nc%d%d%d" % (b, hc, jp),
+                    k_view(b, hc)[:, :, js, 64:128].rearrange("p h j d -> p j h d"),
+                    tiles["pn%d%d%d" % (b, hc, jp)][:].rearrange("p (j h d) -> p j h d", j=2, h=4),
                 )
-                nc.scalar.copy(
-                    out=k4[:, :, js, 64:128].rearrange("p h j d -> p j h d"),
-                    in_=pn[:].rearrange("p (j h d) -> p j h d", j=2, h=4),
-                )
-            for s in range(2):
-                nc.vector.tensor_tensor(
+
+            return run
+
+        def make_a(s, b, hc):
+            def run():
+                k4 = k_view(b, hc)
+                t4 = t_view(b, hc)
+                nc.gpsimd.tensor_tensor(
                     out=k4[:, :, :, 32 * s : 32 * s + 32],
                     in0=k4[:, :, :, 32 * s : 32 * s + 32],
                     in1=t4[:, :, :, 32 - 32 * s : 64 - 32 * s],
                     op=ADD,
                 )
-            nc.sync.dma_start(
-                out=out_0[b, 4 * hc : 4 * hc + 4].rearrange("h (p j) d -> p h (j d)", j=4),
-                in_=ksb[:].rearrange("p (h f) -> p h f", h=4),
-            )
 
-        x_tiles(0)
-        kvq = [
-            weight_unit(
-                kv_raw[g // 2][:].rearrange("p (g t n) -> p g t n", g=2, t=4)[:, g % 2, :, :],
-                "kv%d" % g,
-            )
-            for g in range(4)
-        ]
-        latent(0)
-        vq = [
-            weight_unit(
-                v_raw[hc // 2][:].rearrange("p (t n) -> p t n", t=4)[:, :, cols(hc % 2, 512)],
-                "v%d" % hc,
-            )
-            for hc in range(4)
-        ]
-        for hc in range(4):
-            v_chunk(0, hc)
-        x_tiles(1)
-        latent(1)
-        nq = [
-            weight_unit(n_raw[:].rearrange("p (t n) -> p t n", t=4)[:, :, cols(h, 512)], "n%d" % h)
-            for h in range(2)
-        ]
-        rq = {}
-        for g in range(4):
-            for h in range(2):
-                rq[(g, h)] = weight_unit(
-                    r_raw[g][:].rearrange("p (t n) -> p t n", t=4)[:, :, cols(h, 512)],
-                    "r%d%d" % (g, h),
-                )
-        for hc in range(4):
-            k_chunk(0, hc)
-            v_chunk(1, hc)
-        for hc in range(4):
-            k_chunk(1, hc)
+            return run
+
+        for b in range(2):
+            for hc in range(4):
+                for j in range(4):
+                    ops["v%d%d%d" % (b, hc, j)] = make_v(b, hc, j)
+                    ops["vc%d%d%d" % (b, hc, j)] = make_vc(b, hc, j)
+                ops["Sv%d%d" % (b, hc)] = make_store(out_1, "vs%d%d" % (b, hc), b, hc)
+                for jp in range(2):
+                    ops["r%d%d%d" % (b, hc, jp)] = make_r(b, hc, jp)
+                    ops["n%d%d%d" % (b, hc, jp)] = make_n(b, hc, jp)
+                    ops["m1%d%d%d" % (b, hc, jp)] = make_m(1, b, hc, jp)
+                    ops["m2%d%d%d" % (b, hc, jp)] = make_m(2, b, hc, jp)
+                    ops["nc%d%d%d" % (b, hc, jp)] = make_nc(b, hc, jp)
+                for s in range(2):
+                    ops["a%d%d%d" % (s, b, hc)] = make_a(s, b, hc)
+                ops["Sk%d%d" % (b, hc)] = make_store(out_0, "ks%d%d" % (b, hc), b, hc)
+
+        assert len(ORDER) == len(ops)
+        for name in ORDER:
+            ops[name]()

@@ -15,37 +15,40 @@ P = 128
 FLOPS = 2 * 1024 * (2048 * 512 + 2048 * 1024 + 512 * 1024 + 512 * 2048)
 
 ON_VECTOR = (
-    "xc40", "nc000", "nc021",
+    "xc11", "xc21", "lc0", "nc000",
 )
 ON_SCALAR = (
-    "WUv2", "WUv3",
+    "WUkv0", "WUkv2", "WUv1", "WUv2", "WUv3", "WUn1",
+)
+ON_GPSIMD = (
+    "a000", "a100", "a110", "a101", "a002", "a112", "a012", "a003",
 )
 ORDER = (
-    "Lx0", "Lx1", "T00", "T01", "xc00", "T10", "Lkv0", "T11", "xc01", "xc10", "XQ0", "xc11", "T20",
-    "T21", "xc20", "XQ1", "T30", "Lkv1", "T31", "xc21", "xc30", "XQ2", "xc31", "WUkv0", "Lx2",
-    "WUkv1", "XQ3", "WUkv2", "Lx3", "WUkv3", "T40", "T41", "WQkv0", "T50", "Lv0", "xc41", "T51",
-    "WQkv1", "xc50", "WQkv2", "xc51", "T60", "WQkv3", "T61", "xc60", "T70", "xc40", "Lr0", "LT0",
-    "xc61", "XQ5", "xc70", "XQ4", "LT1", "lc0", "WUv0", "Lr1", "LT2", "lc1", "WUv1", "LT3", "WQv0",
-    "lc2", "XQ6", "Lr2", "T71", "WQv1", "lc3", "LT4", "WUr00", "xc71", "LT5", "lc4", "LQ0", "Lr3",
-    "XQ7", "v000", "lc5", "WUr10", "v001", "v002", "vc000", "v003", "LT6", "vc001", "WUr20", "Ln0",
-    "vc002", "LT7", "vc003", "WQr00", "lc6", "WUr30", "v010", "lc7", "Lv1", "v011", "v012",
-    "WQr10", "vc010", "v013", "LQ1", "vc011", "WQr20", "vc012", "v100", "v101", "WQr30", "vc013",
-    "v102", "Sv00", "v103", "vc100", "WUn0", "v110", "v111", "vc101", "v112", "v113", "vc102",
-    "WUr01", "r000", "vc103", "Sv01", "vc110", "WQn0", "r001", "vc111", "m1000", "vc112", "m2000",
-    "n000", "n001", "vc113", "m1001", "r100", "nc001", "m2001", "Sv10", "WUv2", "r101", "nc000",
-    "a000", "m1100", "n100", "m2100", "a100", "n101", "r010", "m1101", "Sv11", "nc100", "m2101",
-    "nc101", "r011", "WQv2", "a010", "WUv3", "m1010", "v020", "m2010", "v021", "a110", "Sk00",
-    "v022", "m1011", "v023", "n010", "m2011", "n011", "vc020", "v120", "WUr11", "v121", "a001",
-    "vc021", "v122", "v123", "vc022", "Sk10", "WUr21", "r110", "vc023", "a101", "nc010", "WUr31",
-    "r111", "nc011", "vc120", "m1110", "Sv02", "n110", "vc121", "n111", "m2110", "vc122", "m1111",
-    "vc123", "m2111", "nc110", "WQv3", "nc111", "a011", "Sk01", "WQr01", "v030", "v031", "WQr11",
-    "vc030", "a111", "v032", "v033", "WQr21", "vc031", "v130", "v131", "vc032", "WQr31", "v132",
-    "Sv12", "v133", "vc033", "WUn1", "r020", "vc130", "vc131", "WQn1", "r021", "vc132", "m1020",
-    "Sk11", "vc133", "m2020", "n020", "n021", "nc020", "m1021", "r120", "m2021", "r121", "nc021",
-    "a002", "Sv03", "m1120", "n120", "m2120", "a102", "n121", "nc120", "r030", "m1121", "nc121",
-    "m2121", "r031", "Sk02", "m1030", "a012", "m2030", "n030", "m1031", "n031", "a112", "nc030",
-    "r130", "m2031", "nc031", "Sv13", "a003", "r131", "m1130", "m2130", "a103", "n130", "m1131",
-    "n131", "nc130", "m2131", "nc131", "Sk12", "a013", "a113", "Sk03", "Sk13",
+    "Lx0", "Lx1", "T11", "T01", "xc11", "T00", "Lkv0", "xc01", "T10", "xc10", "xc00", "T20", "T21",
+    "xc20", "T30", "xc21", "Lkv1", "T31", "xc30", "XQ0", "xc31", "WUkv0", "WUkv1", "Lx2", "XQ1",
+    "XQ2", "WUkv2", "WUkv3", "Lx3", "WQkv0", "WQkv1", "T51", "WQkv3", "T40", "xc51", "T41", "Lv0",
+    "WQkv2", "T50", "xc40", "XQ3", "xc50", "xc41", "T60", "XQ5", "T61", "xc60", "LT0", "XQ4",
+    "Lr0", "xc61", "T70", "lc0", "LT1", "xc70", "WUv0", "WUv1", "Lr1", "LT2", "XQ6", "WQv0", "LT3",
+    "WUr00", "lc2", "Lr2", "T71", "WQv1", "lc3", "LT4", "lc1", "WQr00", "xc71", "LQ0", "LT5",
+    "lc4", "Lr3", "WUr10", "v001", "lc5", "v000", "XQ7", "v002", "vc000", "v003", "WQr10", "LT6",
+    "vc001", "Ln0", "WUr20", "vc002", "LT7", "lc6", "WUr30", "vc003", "v010", "lc7", "Lv1", "v012",
+    "v011", "vc010", "LQ1", "v013", "vc011", "WQr20", "v100", "vc013", "v101", "WQr30", "v113",
+    "vc012", "v111", "WUn0", "Sv00", "v103", "vc100", "v110", "v102", "vc103", "r001", "WUr01",
+    "vc102", "vc101", "v112", "WQn0", "r000", "Sv01", "vc113", "m2001", "vc111", "m1001", "n000",
+    "vc110", "r100", "m2000", "vc112", "m1000", "WUv2", "n001", "Sv10", "r101", "nc000", "a000",
+    "m2100", "n100", "m1100", "a100", "r011", "m2101", "nc100", "Sv11", "m1101", "nc001", "r010",
+    "WQv2", "WUv3", "WUr11", "n101", "v022", "v020", "n010", "a010", "Sk00", "r110", "vc020",
+    "m2011", "a110", "nc101", "m2010", "v023", "v021", "vc022", "m1010", "n110", "v120", "nc010",
+    "m1011", "v122", "Sk10", "v121", "vc021", "WQv3", "nc110", "WUr21", "v133", "vc023", "r111",
+    "vc120", "m1110", "a101", "Sv02", "vc121", "n011", "m2110", "v130", "vc122", "n111", "m2111",
+    "v033", "nc011", "v131", "a001", "v132", "WUn1", "v123", "WQr01", "Sk01", "m1111", "v030",
+    "WUr31", "vc123", "WQr11", "v032", "vc130", "WQr21", "Sv12", "vc032", "WQr31", "nc111", "a011",
+    "vc033", "r020", "a111", "vc030", "vc131", "Sk11", "v031", "m1020", "r021", "vc031", "WQn1",
+    "vc133", "m2020", "n020", "r120", "m1021", "nc020", "Sv03", "m2021", "vc132", "r121", "m2120",
+    "a002", "m1120", "r030", "m1121", "m2121", "Sv13", "n021", "a102", "r031", "nc021", "m2030",
+    "a112", "n121", "m1031", "n031", "n120", "a012", "Sk02", "m2031", "n030", "nc120", "r130",
+    "m1030", "nc121", "a103", "nc031", "r131", "m2130", "a003", "nc030", "Sk12", "n130", "m1131",
+    "n131", "nc131", "m2131", "nc130", "m1130", "a113", "Sk03", "a013", "Sk13",
 )
 
 
@@ -323,7 +326,8 @@ def tile_multiheadlatentattention_pb_kernel(
             def run():
                 k4 = k_view(b, hc)
                 t4 = t_view(b, hc)
-                nc.gpsimd.tensor_tensor(
+                engine = nc.gpsimd if ("a%d%d%d" % (s, b, hc)) in ON_GPSIMD else nc.vector
+                engine.tensor_tensor(
                     out=k4[:, :, :, 32 * s : 32 * s + 32],
                     in0=k4[:, :, :, 32 * s : 32 * s + 32],
                     in1=t4[:, :, :, 32 - 32 * s : 64 - 32 * s],

@@ -14,43 +14,6 @@ ADD = mybir.AluOpType.add
 P = 128
 FLOPS = 2 * 1024 * (2048 * 512 + 2048 * 1024 + 512 * 1024 + 512 * 2048)
 
-ON_VECTOR = (
-    "xc11", "xc21", "lc0", "nc000",
-)
-ON_SCALAR = (
-    "WUkv0", "WUkv2", "WUv1", "WUv2", "WUv3", "WUn1",
-)
-ON_GPSIMD = (
-    "a000", "a100", "a110", "a101", "a002", "a112", "a012", "a003",
-)
-ORDER = (
-    "Lx0", "Lx1", "T11", "T01", "xc11", "T00", "Lkv0", "xc01", "T10", "xc10", "xc00", "T20", "T21",
-    "xc20", "T30", "xc21", "Lkv1", "T31", "xc30", "XQ0", "xc31", "WUkv0", "WUkv1", "Lx2", "XQ1",
-    "XQ2", "WUkv2", "WUkv3", "Lx3", "WQkv0", "WQkv1", "T51", "WQkv3", "T40", "xc51", "T41", "Lv0",
-    "WQkv2", "T50", "xc40", "XQ3", "xc50", "xc41", "T60", "XQ5", "T61", "xc60", "LT0", "XQ4",
-    "Lr0", "xc61", "T70", "lc0", "LT1", "xc70", "WUv0", "WUv1", "Lr1", "LT2", "XQ6", "WQv0", "LT3",
-    "WUr00", "lc2", "Lr2", "T71", "WQv1", "lc3", "LT4", "lc1", "WQr00", "xc71", "LQ0", "LT5",
-    "lc4", "Lr3", "WUr10", "v001", "lc5", "v000", "XQ7", "v002", "vc000", "v003", "WQr10", "LT6",
-    "vc001", "Ln0", "WUr20", "vc002", "LT7", "lc6", "WUr30", "vc003", "v010", "lc7", "Lv1", "v012",
-    "v011", "vc010", "LQ1", "v013", "vc011", "WQr20", "v100", "vc013", "v101", "WQr30", "v113",
-    "vc012", "v111", "WUn0", "Sv00", "v103", "vc100", "v110", "v102", "vc103", "r001", "WUr01",
-    "vc102", "vc101", "v112", "WQn0", "r000", "Sv01", "vc113", "m2001", "vc111", "m1001", "n000",
-    "vc110", "r100", "m2000", "vc112", "m1000", "WUv2", "n001", "Sv10", "r101", "nc000", "a000",
-    "m2100", "n100", "m1100", "a100", "r011", "m2101", "nc100", "Sv11", "m1101", "nc001", "r010",
-    "WQv2", "WUv3", "WUr11", "n101", "v022", "v020", "n010", "a010", "Sk00", "r110", "vc020",
-    "m2011", "a110", "nc101", "m2010", "v023", "v021", "vc022", "m1010", "n110", "v120", "nc010",
-    "m1011", "v122", "Sk10", "v121", "vc021", "WQv3", "nc110", "WUr21", "v133", "vc023", "r111",
-    "vc120", "m1110", "a101", "Sv02", "vc121", "n011", "m2110", "v130", "vc122", "n111", "m2111",
-    "v033", "nc011", "v131", "a001", "v132", "WUn1", "v123", "WQr01", "Sk01", "m1111", "v030",
-    "WUr31", "vc123", "WQr11", "v032", "vc130", "WQr21", "Sv12", "vc032", "WQr31", "nc111", "a011",
-    "vc033", "r020", "a111", "vc030", "vc131", "Sk11", "v031", "m1020", "r021", "vc031", "WQn1",
-    "vc133", "m2020", "n020", "r120", "m1021", "nc020", "Sv03", "m2021", "vc132", "r121", "m2120",
-    "a002", "m1120", "r030", "m1121", "m2121", "Sv13", "n021", "a102", "r031", "nc021", "m2030",
-    "a112", "n121", "m1031", "n031", "n120", "a012", "Sk02", "m2031", "n030", "nc120", "r130",
-    "m1030", "nc121", "a103", "nc031", "r131", "m2130", "a003", "nc030", "Sk12", "n130", "m1131",
-    "n131", "nc131", "m2131", "nc130", "m1130", "a113", "Sk03", "a013", "Sk13",
-)
-
 
 def tile_multiheadlatentattention_pb_kernel(
     tc, x, Wkv_d, Wk_nope, Wv_u, Wrk, cos, sin, out_0, out_1
@@ -69,16 +32,26 @@ def tile_multiheadlatentattention_pb_kernel(
         make_identity(nc, ident[:])
         cos_b = const.tile([P, 4, 64], BF16, name="cos_b")
         sin_b = const.tile([P, 4, 64], BF16, name="sin_b")
-        nc.scalar.dma_start(out=cos_b[:], in_=cos.rearrange("(p j) d -> p j d", j=4))
-        nc.scalar.dma_start(out=sin_b[:], in_=sin.rearrange("(p j) d -> p j d", j=4))
-        cosf = const.tile([P, 4, 64], F32, name="cosf")
-        sinsw = const.tile([P, 4, 64], F32, name="sinsw")
-        nc.vector.tensor_copy(out=cosf[:], in_=cos_b[:])
-        nc.vector.tensor_copy(out=sinsw[:, :, 0:32], in_=sin_b[:, :, 32:64])
-        nc.vector.tensor_scalar_mul(out=sinsw[:, :, 32:64], in0=sin_b[:, :, 0:32], scalar1=-1.0)
+        def load_tables():
+            nc.sync.dma_start(out=cos_b[:], in_=cos.rearrange("(p j) d -> p j d", j=4))
+            nc.sync.dma_start(out=sin_b[:], in_=sin.rearrange("(p j) d -> p j d", j=4))
+
+        sinsw = const.tile([P, 4, 64], BF16, name="sinsw")
+
+        def prep_tables():
+            nc.vector.tensor_copy(out=sinsw[:, :, 0:32], in_=sin_b[:, :, 32:64])
+            nc.vector.tensor_scalar_mul(out=sinsw[:, :, 32:64], in0=sin_b[:, :, 0:32], scalar1=-1.0)
 
         tiles = {}
         ops = {}
+        engine_of = ["s"]
+
+        def do(name, engine="s"):
+            engine_of[0] = engine
+            emitted.append(name)
+            ops[name]()
+
+        emitted = []
 
         def cols(i, w):
             return slice(i * w, i * w + w)
@@ -99,7 +72,7 @@ def tile_multiheadlatentattention_pb_kernel(
             return tiles[key]
 
         def copy(name, out, in_):
-            if name in ON_VECTOR:
+            if engine_of[0] == "v":
                 nc.vector.tensor_copy(out=out, in_=in_)
             else:
                 nc.scalar.copy(out=out, in_=in_)
@@ -193,7 +166,7 @@ def tile_multiheadlatentattention_pb_kernel(
                 src = pick(tiles[rawkey][:])
                 dst = grp_tile("g" + label)[:].rearrange("p (c i t) -> p c t i", i=4, t=4)
                 s = src.rearrange("p t (c i) -> p c t i", i=4)
-                if ("WU" + label) in ON_SCALAR:
+                if engine_of[0] == "s":
                     nc.scalar.copy(out=dst, in_=s)
                 else:
                     nc.vector.tensor_copy(out=dst, in_=s)
@@ -298,7 +271,7 @@ def tile_multiheadlatentattention_pb_kernel(
                 r4 = tiles["pr%d%d%d" % (b, hc, jp)][:].rearrange("p (j h d) -> p j h d", j=2, h=4)
                 if which == 1:
                     out = k_view(b, hc)[:, :, js, 0:64]
-                    table = cosf
+                    table = cos_b
                 else:
                     out = t_view(b, hc)[:, :, js, :]
                     table = sinsw
@@ -326,7 +299,7 @@ def tile_multiheadlatentattention_pb_kernel(
             def run():
                 k4 = k_view(b, hc)
                 t4 = t_view(b, hc)
-                engine = nc.gpsimd if ("a%d%d%d" % (s, b, hc)) in ON_GPSIMD else nc.vector
+                engine = nc.gpsimd if engine_of[0] == "g" else nc.vector
                 engine.tensor_tensor(
                     out=k4[:, :, :, 32 * s : 32 * s + 32],
                     in0=k4[:, :, :, 32 * s : 32 * s + 32],
@@ -352,6 +325,105 @@ def tile_multiheadlatentattention_pb_kernel(
                     ops["a%d%d%d" % (s, b, hc)] = make_a(s, b, hc)
                 ops["Sk%d%d" % (b, hc)] = make_store(out_0, "ks%d%d" % (b, hc), b, hc)
 
-        assert len(ORDER) == len(ops)
-        for name in ORDER:
-            ops[name]()
+        def w(labels):
+            for label in labels:
+                do("WU" + label, "v")
+            for label in labels:
+                do("WQ" + label)
+
+        def v(b, hc):
+            for j in range(4):
+                do("v%d%d%d" % (b, hc, j))
+                do("vc%d%d%d" % (b, hc, j), "s")
+            do("Sv%d%d" % (b, hc))
+
+        def k(b, hc, engine):
+            for jp in range(2):
+                s = "%d%d%d" % (b, hc, jp)
+                do("r" + s)
+                do("n" + s)
+                do("nc" + s, "s")
+                do("m1" + s)
+                do("m2" + s)
+            for s in range(2):
+                do("a%d%d%d" % (s, b, hc), engine)
+            do("Sk%d%d" % (b, hc))
+
+        for label in ("kv0", "x0", "kv1", "x1", "x2", "x3", "v0", "v1", "r0", "r1", "n0", "r2", "r3"):
+            do("L" + label)
+            if label == "v0":
+                load_tables()
+        do("WUkv0", "v")
+        do("WUkv1", "s")
+        do("WQkv0")
+        do("WQkv1")
+        for i in range(2):
+            for h in range(2):
+                do("T%d%d" % (i, h))
+                do("xc%d%d" % (i, h), "sv"[h])
+        do("XQ0")
+        do("WUkv2", "v")
+        do("WUkv3", "v")
+        do("XQ1")
+        do("WQkv2")
+        do("WQkv3")
+        for i in range(2, 4):
+            for h in range(2):
+                do("T%d%d" % (i, h))
+                do("xc%d%d" % (i, h), "s")
+            do("XQ%d" % i)
+        for i in range(4):
+            do("LT%d" % i)
+            for h in range(2):
+                do("T%d%d" % (4 + i, h))
+                do("xc%d%d" % (4 + i, h), "s")
+            do("lc%d" % i, "s")
+            if i < 2:
+                do("WUv%d" % i, "v")
+            else:
+                do("WQv%d" % (i - 2))
+            do("XQ%d" % (4 + i))
+        do("LQ0")
+        do("WUv2", "v")
+        do("LT4")
+        do("lc4", "s")
+        do("LT5")
+        do("lc5", "s")
+        do("LT6")
+        do("lc6", "s")
+        v(0, 0)
+        do("LT7")
+        do("lc7", "s")
+        do("WQv2")
+        v(0, 1)
+        do("WUr00", "v")
+        do("WUv3", "v")
+        do("LQ1")
+        prep_tables()
+        do("WQr00")
+        w(("r10",))
+        do("WUn0", "s")
+        v(1, 0)
+        w(("r20", "r30"))
+        do("WQv3")
+        v(1, 1)
+        v(0, 2)
+        do("WQn0")
+        v(1, 2)
+        w(("r01",))
+        k(0, 0, "g")
+        v(0, 3)
+        w(("r11",))
+        do("WUr21", "s")
+        k(1, 0, "g")
+        do("WUn1", "s")
+        v(1, 3)
+        w(("r31",))
+        do("WQr21")
+        k(0, 1, "g")
+        k(1, 1, "g")
+        do("WQn1")
+        for hc in range(2, 4):
+            for b in range(2):
+                k(b, hc, "v" if hc == 3 else "g")
+        assert len(set(emitted)) == len(emitted) == len(ops), set(ops) - set(emitted)

@@ -21,7 +21,8 @@ def tile_multiheadlatentattention_pb_kernel(
     nc = tc.nc
     with ExitStack() as ctx:
         const = ctx.enter_context(tc.tile_pool(name="const", bufs=1))
-        big = ctx.enter_context(tc.tile_pool(name="big", bufs=13))
+        big = ctx.enter_context(tc.tile_pool(name="big", bufs=12))
+        vraw = ctx.enter_context(tc.tile_pool(name="vraw", bufs=1))
         grp = ctx.enter_context(tc.tile_pool(name="grp", bufs=6))
         keep = ctx.enter_context(tc.tile_pool(name="keep", bufs=1))
         tmpp = ctx.enter_context(tc.tile_pool(name="tmpp", bufs=2))
@@ -32,62 +33,86 @@ def tile_multiheadlatentattention_pb_kernel(
         make_identity(nc, ident[:])
         cos_b = const.tile([P, 4, 64], BF16, name="cos_b")
         sin_b = const.tile([P, 4, 64], BF16, name="sin_b")
-        def load_tables():
-            nc.sync.dma_start(out=cos_b[:], in_=cos.rearrange("(p j) d -> p j d", j=4))
-            nc.sync.dma_start(out=sin_b[:], in_=sin.rearrange("(p j) d -> p j d", j=4))
+        sin_sw = const.tile([P, 4, 64], BF16, name="sin_sw")
 
-        sinsw = const.tile([P, 4, 64], BF16, name="sinsw")
-
-        def prep_tables():
-            nc.vector.tensor_copy(out=sinsw[:, :, 0:32], in_=sin_b[:, :, 32:64])
-            nc.vector.tensor_scalar_mul(out=sinsw[:, :, 32:64], in0=sin_b[:, :, 0:32], scalar1=-1.0)
-
-        tiles = {}
-        ops = {}
-        engine_of = ["s"]
-
-        def do(name, engine="s"):
-            engine_of[0] = engine
-            emitted.append(name)
-            ops[name]()
-
-        emitted = []
+        raws = {}
+        groups = {}
+        quants = {}
+        banks = {}
+        outs = {}
+        tms = {}
 
         def cols(i, w):
             return slice(i * w, i * w + w)
 
-        def big_tile(key, dtype, width):
-            if key not in tiles:
-                tiles[key] = big.tile([P, width], dtype, tag="big", name=key)
-            return tiles[key]
+        def load_x(c, parts=1):
+            rows = x[c // 2].rearrange("(p j) k -> p j k", j=4)
+            raws["x%d" % c] = big.tile([P, 4096], BF16, tag="big", name="rawx%d" % c)
+            dst = raws["x%d" % c][:].rearrange("p (j k) -> p j k", j=2)
+            for i in range(parts):
+                js = cols(i, 2 // parts)
+                nc.sync.dma_start(out=dst[:, js, :], in_=rows[:, 2 * (c % 2) : 2 * (c % 2) + 2, :][:, js, :])
 
-        def grp_tile(key):
-            if key not in tiles:
-                tiles[key] = grp.tile([P, 2048], BF16, tag="g", name=key, align_bytes=64)
-            return tiles[key]
+        def load_kv(c, parts=1):
+            raws["kv%d" % c] = big.tile([P, 4096], BF16, tag="big", name="rawkv%d" % c)
+            src = Wkv_d[1024 * c : 1024 * c + 1024, :].rearrange("(g u p e) n -> p (g u) (e n)", g=2, u=2, p=P, e=2)
+            dst = raws["kv%d" % c][:].rearrange("p (a f) -> p a f", a=4)
+            for i in range(parts):
+                part = cols(i, 4 // parts)
+                nc.sync.dma_start(out=dst[:, part, :], in_=src[:, part, :])
 
-        def ps_tile(key):
-            if key not in tiles:
-                tiles[key] = psum.tile([P, 512], F32, tag="ps", name=key)
-            return tiles[key]
+        def load_v():
+            raws["v"] = vraw.tile([P, 8192], BF16, name="rawv")
+            for c in range(2):
+                nc.sync.dma_start(
+                    out=raws["v"][:, cols(c, 4096)].rearrange("p (t n) -> p t n", t=2),
+                    in_=Wv_u.rearrange("(p t) n -> p t n", t=4)[:, cols(c, 2), :],
+                )
 
-        def copy(name, out, in_):
-            if engine_of[0] == "v":
+        def load_n():
+            raws["n"] = big.tile([P, 4096], BF16, tag="big", name="rawn")
+            nc.sync.dma_start(out=raws["n"][:].rearrange("p (t n) -> p t n", t=4), in_=Wk_nope.rearrange("(p t) n -> p t n", t=4))
+
+        def load_r(g):
+            raws["r%d" % g] = big.tile([P, 4096], BF16, tag="big", name="rawr%d" % g)
+            nc.sync.dma_start(
+                out=raws["r%d" % g][:].rearrange("p (u f) -> p u f", u=2),
+                in_=Wrk[512 * g : 512 * g + 512, :].rearrange("(u p e) n -> p u (e n)", u=2, p=P, e=2),
+            )
+
+        def load_tables():
+            nc.sync.dma_start(out=cos_b[:], in_=cos.rearrange("(p j) d -> p j d", j=4))
+            nc.sync.dma_start(out=sin_b[:], in_=sin.rearrange("(p j) d -> p j d", j=4))
+
+        def prep_tables():
+            nc.vector.tensor_copy(out=sin_sw[:, :, 0:32], in_=sin_b[:, :, 32:64])
+            nc.vector.tensor_scalar_mul(out=sin_sw[:, :, 32:64], in0=sin_b[:, :, 0:32], scalar1=-1.0)
+
+        def copy(engine, out, in_):
+            if engine == "v":
                 nc.vector.tensor_copy(out=out, in_=in_)
             else:
                 nc.scalar.copy(out=out, in_=in_)
 
-        def quantise(gkey, label):
-            codes = keep.tile([P, 512], U32, name="c_" + label, align_bytes=64)
-            scales = keep.tile([P, 512], U8, name="s_" + label, align_bytes=64)
-            nc.vector.quantize_mx(
-                out=codes[:].bitcast(FP8X4), scales=scales[:], in_=tiles[gkey][:]
-            )
-            tiles["q" + label] = (codes, scales)
+        def bank(key):
+            banks[key] = psum.tile([P, 512], F32, tag="ps", name="ps" + key)
+            return banks[key]
+
+        def group(key):
+            if key not in groups:
+                groups[key] = grp.tile([P, 2048], BF16, tag="g", name="g" + key, align_bytes=64)
+            return groups[key]
+
+        def quantise(*keys):
+            for key in keys:
+                codes = keep.tile([P, 512], U32, name="c_" + key, align_bytes=64)
+                scales = keep.tile([P, 512], U8, name="s_" + key, align_bytes=64)
+                nc.vector.quantize_mx(out=codes[:].bitcast(FP8X4), scales=scales[:], in_=groups[key][:])
+                quants[key] = (codes, scales)
 
         def mx(out, a, acols, b, bcols, start, stop):
-            qa = tiles["q" + a]
-            qb = tiles["q" + b]
+            qa = quants[a]
+            qb = quants[b]
             nc.tensor.matmul_mx(
                 out=out,
                 lhsT=qa[0][:, acols].bitcast(FP8X4),
@@ -98,183 +123,86 @@ def tile_multiheadlatentattention_pb_kernel(
                 stop=stop,
             )
 
-        views = {}
-        for c in range(4):
-            views["x%d" % c] = x[c // 2].rearrange("(p j) k -> p j k", j=4)[
-                :, 2 * (c % 2) : 2 * (c % 2) + 2, :
-            ]
-            views["r%d" % c] = Wrk[512 * c : 512 * c + 512, :].rearrange(
-                "(u p e) n -> p u (e n)", u=2, p=P, e=2
-            )
-        for c in range(2):
-            views["kv%d" % c] = Wkv_d[1024 * c : 1024 * c + 1024, :].rearrange(
-                "(g u p e) n -> p (g u) (e n)", g=2, u=2, p=P, e=2
-            )
-            views["v%d" % c] = Wv_u.rearrange("(t p) n -> p t n", t=4)[
-                :, :, 1024 * c : 1024 * c + 1024
-            ]
-        views["n0"] = Wk_nope.rearrange("(t p) n -> p t n", t=4)
-
-        def make_load(label):
-            def run():
-                view = views[label]
-                raw = big_tile("raw" + label, BF16, 4096)
-                nc.sync.dma_start(
-                    out=raw[:].rearrange("p (a f) -> p a f", a=view.shape[1]), in_=view
-                )
-
-            return run
-
-        for label in views:
-            ops["L" + label] = make_load(label)
-
-        def make_t(i, h):
-            def run():
-                xw = tiles["rawx%d" % (i // 2)][:].bitcast(F32)
-                xt3 = ps_tile("px%d%d" % (i, h))[:].rearrange("p (a r) -> p a r", a=4)
+        def x_in(i, engines="ss"):
+            xw = raws["x%d" % (i // 2)][:].bitcast(F32)
+            gw = group("x%d" % i)[:].bitcast(F32).rearrange("p (g r u) -> p g r u", g=4, u=2)
+            for h in range(2):
+                xt = bank("x%d%d" % (i, h))
+                xt3 = xt[:].rearrange("p (a r) -> p a r", a=4)
                 for a in range(4):
                     c0 = 1024 * (i % 2) + 512 * h + 128 * a
                     nc.tensor.transpose(xt3[:, a, :], xw[:, c0 : c0 + 128], ident[:])
+                copy(engines[h], gw[:, 2 * h : 2 * h + 2, :, :], xt[:].rearrange("p (g u r) -> p g r u", g=2, u=2))
 
-            return run
-
-        def make_xc(i, h):
-            def run():
-                gw = grp_tile("gx%d" % i)[:].bitcast(F32).rearrange("p (g r u) -> p g r u", g=4, u=2)
-                copy(
-                    "xc%d%d" % (i, h),
-                    gw[:, 2 * h : 2 * h + 2, :, :],
-                    tiles["px%d%d" % (i, h)][:].rearrange("p (g u r) -> p g r u", g=2, u=2),
-                )
-
-            return run
-
-        def make_q(gkey, label):
-            def run():
-                quantise(gkey, label)
-
-            return run
-
-        for i in range(8):
-            for h in range(2):
-                ops["T%d%d" % (i, h)] = make_t(i, h)
-                ops["xc%d%d" % (i, h)] = make_xc(i, h)
-            ops["XQ%d" % i] = make_q("gx%d" % i, "x%d" % i)
-
-        def make_wu(label, rawkey, pick):
-            def run():
-                src = pick(tiles[rawkey][:])
-                dst = grp_tile("g" + label)[:].rearrange("p (c i t) -> p c t i", i=4, t=4)
-                s = src.rearrange("p t (c i) -> p c t i", i=4)
-                if engine_of[0] == "s":
-                    nc.scalar.copy(out=dst, in_=s)
+        def w_copy(engine, *labels):
+            for label in labels:
+                kind = label[: len(label) - 1]
+                i = int(label[len(label) - 1])
+                dst = group(label)[:]
+                if kind == "kv":
+                    src = raws["kv%d" % (i // 2)][:].rearrange("p (g t n) -> p g t n", g=2, t=4)[:, i % 2, :, :]
+                    copy(engine, dst.rearrange("p (t m j) -> p t m j", t=4, j=4), src.rearrange("p j (m t) -> p t m j", t=4))
                 else:
-                    nc.vector.tensor_copy(out=dst, in_=s)
+                    src = raws[kind][:].rearrange("p (t n) -> p t n", t=4)[:, :, cols(i, 512)]
+                    copy(engine, dst.rearrange("p (c i t) -> p c t i", i=4, t=4), src.rearrange("p t (c i) -> p c t i", i=4))
 
-            return run
+        def latent(i, engine="s"):
+            pl = bank("l%d" % i)
+            pl3 = pl[:].rearrange("p (t r) -> p t r", t=4)
+            for t in range(4):
+                for g in range(4):
+                    mx(pl3[:, t, :], "kv%d" % g, cols(t, 128), "x%d" % i, cols(g, 128), g == 0, g == 3)
+            g4 = group("l%d" % (i // 4))[:].rearrange("p (j r t) -> p j r t", j=4, t=4)
+            copy(engine, g4[:, i % 4, :, :], pl[:].rearrange("p (t r) -> p r t", t=4))
 
-        def pick_kv(g):
-            return lambda ap: ap.rearrange("p (g t n) -> p g t n", g=2, t=4)[:, g, :, :]
+        def out_tile(key):
+            if key not in outs:
+                outs[key] = big.tile([P, 2048], F32, tag="big", name="o" + key)
+            return outs[key][:].rearrange("p (h j d) -> p h j d", h=4, j=4)
 
-        def pick_half(h):
-            return lambda ap: ap.rearrange("p (t n) -> p t n", t=4)[:, :, cols(h, 512)]
+        def store(dram, key, b, hc):
+            nc.sync.dma_start(
+                out=dram[b, 4 * hc : 4 * hc + 4].rearrange("h (p j) d -> p h (j d)", j=4),
+                in_=outs[key][:].rearrange("p (h f) -> p h f", h=4),
+            )
 
-        units = []
-        for g in range(4):
-            units.append(("kv%d" % g, "rawkv%d" % (g // 2), pick_kv(g % 2)))
-            units.append(("v%d" % g, "rawv%d" % (g // 2), pick_half(g % 2)))
-            for h in range(2):
-                units.append(("r%d%d" % (g, h), "rawr%d" % g, pick_half(h)))
-        for h in range(2):
-            units.append(("n%d" % h, "rawn0", pick_half(h)))
-        for label, rawkey, pick in units:
-            ops["WU" + label] = make_wu(label, rawkey, pick)
-            ops["WQ" + label] = make_q("g" + label, label)
+        def v(b, hc, js=range(4)):
+            key = "v%d%d" % (b, hc)
+            for j in js:
+                pv = bank("%s%d" % (key, j))
+                mx(pv[:], "l%d" % b, cols(j, 128), "v%d" % hc, cols(0, 512), True, True)
+                copy("s", out_tile(key)[:, :, j, :], pv[:].rearrange("p (h d) -> p h d", h=4))
+            if 3 in js:
+                store(out_1, key, b, hc)
 
-        def make_lt(i):
-            def run():
-                pl3 = ps_tile("pl%d" % i)[:].rearrange("p (t r) -> p t r", t=4)
-                for t in range(4):
-                    for g in range(4):
-                        mx(pl3[:, t, :], "kv%d" % g, cols(t, 128), "x%d" % i, cols(g, 128), g == 0, g == 3)
+        def r_matmul(b, hc, jp):
+            pr3 = bank("r%d%d%d" % (b, hc, jp))[:].rearrange("p (j n) -> p j n", j=2)
+            for jj in range(2):
+                for g in range(4):
+                    mx(pr3[:, jj, :], "x%d" % (4 * b + 2 * jp + jj), cols(g, 128), "r%d%d" % (g, hc // 2), cols(hc % 2, 256), g == 0, g == 3)
 
-            return run
+        def n_part(b, hc, jp):
+            pn = bank("n%d%d%d" % (b, hc, jp))
+            pn3 = pn[:].rearrange("p (j n) -> p j n", j=2)
+            for jj in range(2):
+                mx(pn3[:, jj, :], "l%d" % b, cols(2 * jp + jj, 128), "n%d" % (hc // 2), cols(hc % 2, 256), True, True)
+            copy(
+                "s",
+                out_tile("k%d%d" % (b, hc))[:, :, cols(jp, 2), 64:128].rearrange("p h j d -> p j h d"),
+                pn[:].rearrange("p (j h d) -> p j h d", j=2, h=4),
+            )
 
-        def make_lc(i):
-            def run():
-                g4 = grp_tile("gl%d" % (i // 4))[:].rearrange("p (j r t) -> p j r t", j=4, t=4)
-                copy("lc%d" % i, g4[:, i % 4, :, :], tiles["pl%d" % i][:].rearrange("p (t r) -> p r t", t=4))
+        def tm_tile(b, hc):
+            key = "t%d%d" % (b, hc)
+            if key not in tms:
+                tms[key] = tmpp.tile([P, 1024], F32, tag="tmp", name=key)
+            return tms[key][:].rearrange("p (h j d) -> p h j d", h=4, j=4)
 
-            return run
-
-        for i in range(8):
-            ops["LT%d" % i] = make_lt(i)
-            ops["lc%d" % i] = make_lc(i)
-        for b in range(2):
-            ops["LQ%d" % b] = make_q("gl%d" % b, "l%d" % b)
-
-        def make_v(b, hc, j):
-            def run():
-                mx(ps_tile("pv%d%d%d" % (b, hc, j))[:], "l%d" % b, cols(j, 128), "v%d" % hc, cols(0, 512), True, True)
-
-            return run
-
-        def make_vc(b, hc, j):
-            def run():
-                v4 = big_tile("vs%d%d" % (b, hc), F32, 2048)[:].rearrange("p (h j d) -> p h j d", h=4, j=4)
-                copy(
-                    "vc%d%d%d" % (b, hc, j),
-                    v4[:, :, j, :],
-                    tiles["pv%d%d%d" % (b, hc, j)][:].rearrange("p (h d) -> p h d", h=4),
-                )
-
-            return run
-
-        def make_store(dram, key, b, hc):
-            def run():
-                nc.sync.dma_start(
-                    out=dram[b, 4 * hc : 4 * hc + 4].rearrange("h (p j) d -> p h (j d)", j=4),
-                    in_=tiles[key][:].rearrange("p (h f) -> p h f", h=4),
-                )
-
-            return run
-
-        def k_view(b, hc):
-            return big_tile("ks%d%d" % (b, hc), F32, 2048)[:].rearrange("p (h j d) -> p h j d", h=4, j=4)
-
-        def t_view(b, hc):
-            key = "tm%d%d" % (b, hc)
-            if key not in tiles:
-                tiles[key] = tmpp.tile([P, 1024], F32, tag="tmp", name=key)
-            return tiles[key][:].rearrange("p (h j d) -> p h j d", h=4, j=4)
-
-        def make_r(b, hc, jp):
-            def run():
-                pr3 = ps_tile("pr%d%d%d" % (b, hc, jp))[:].rearrange("p (j n) -> p j n", j=2)
-                for jj in range(2):
-                    for g in range(4):
-                        mx(pr3[:, jj, :], "x%d" % (4 * b + 2 * jp + jj), cols(g, 128), "r%d%d" % (g, hc // 2), cols(hc % 2, 256), g == 0, g == 3)
-
-            return run
-
-        def make_n(b, hc, jp):
-            def run():
-                pn3 = ps_tile("pn%d%d%d" % (b, hc, jp))[:].rearrange("p (j n) -> p j n", j=2)
-                for jj in range(2):
-                    mx(pn3[:, jj, :], "l%d" % b, cols(2 * jp + jj, 128), "n%d" % (hc // 2), cols(hc % 2, 256), True, True)
-
-            return run
-
-        def make_m(which, b, hc, jp):
-            def run():
-                js = slice(2 * jp, 2 * jp + 2)
-                r4 = tiles["pr%d%d%d" % (b, hc, jp)][:].rearrange("p (j h d) -> p j h d", j=2, h=4)
-                if which == 1:
-                    out = k_view(b, hc)[:, :, js, 0:64]
-                    table = cos_b
-                else:
-                    out = t_view(b, hc)[:, :, js, :]
-                    table = sinsw
+        def rotate(b, hc, jp):
+            js = cols(jp, 2)
+            r4 = banks["r%d%d%d" % (b, hc, jp)][:].rearrange("p (j h d) -> p j h d", j=2, h=4)
+            k4 = out_tile("k%d%d" % (b, hc))
+            for out, table in ((k4[:, :, js, 0:64], cos_b), (tm_tile(b, hc)[:, :, js, :], sin_sw)):
                 nc.vector.tensor_tensor(
                     out=out.rearrange("p h j d -> p j h d"),
                     in0=r4,
@@ -282,148 +210,109 @@ def tile_multiheadlatentattention_pb_kernel(
                     op=MULT,
                 )
 
-            return run
-
-        def make_nc(b, hc, jp):
-            def run():
-                js = slice(2 * jp, 2 * jp + 2)
-                copy(
-                    "nc%d%d%d" % (b, hc, jp),
-                    k_view(b, hc)[:, :, js, 64:128].rearrange("p h j d -> p j h d"),
-                    tiles["pn%d%d%d" % (b, hc, jp)][:].rearrange("p (j h d) -> p j h d", j=2, h=4),
-                )
-
-            return run
-
-        def make_a(s, b, hc):
-            def run():
-                k4 = k_view(b, hc)
-                t4 = t_view(b, hc)
-                engine = nc.gpsimd if engine_of[0] == "g" else nc.vector
-                engine.tensor_tensor(
+        def k_add(b, hc, engine):
+            k4 = out_tile("k%d%d" % (b, hc))
+            t4 = tm_tile(b, hc)
+            for s in range(2):
+                (nc.gpsimd if engine == "g" else nc.vector).tensor_tensor(
                     out=k4[:, :, :, 32 * s : 32 * s + 32],
                     in0=k4[:, :, :, 32 * s : 32 * s + 32],
                     in1=t4[:, :, :, 32 - 32 * s : 64 - 32 * s],
                     op=ADD,
                 )
 
-            return run
-
-        for b in range(2):
-            for hc in range(4):
-                for j in range(4):
-                    ops["v%d%d%d" % (b, hc, j)] = make_v(b, hc, j)
-                    ops["vc%d%d%d" % (b, hc, j)] = make_vc(b, hc, j)
-                ops["Sv%d%d" % (b, hc)] = make_store(out_1, "vs%d%d" % (b, hc), b, hc)
-                for jp in range(2):
-                    ops["r%d%d%d" % (b, hc, jp)] = make_r(b, hc, jp)
-                    ops["n%d%d%d" % (b, hc, jp)] = make_n(b, hc, jp)
-                    ops["m1%d%d%d" % (b, hc, jp)] = make_m(1, b, hc, jp)
-                    ops["m2%d%d%d" % (b, hc, jp)] = make_m(2, b, hc, jp)
-                    ops["nc%d%d%d" % (b, hc, jp)] = make_nc(b, hc, jp)
-                for s in range(2):
-                    ops["a%d%d%d" % (s, b, hc)] = make_a(s, b, hc)
-                ops["Sk%d%d" % (b, hc)] = make_store(out_0, "ks%d%d" % (b, hc), b, hc)
-
-        def w(labels):
-            for label in labels:
-                do("WU" + label, "v")
-            for label in labels:
-                do("WQ" + label)
-
-        def v(b, hc):
-            for j in range(4):
-                do("v%d%d%d" % (b, hc, j))
-                do("vc%d%d%d" % (b, hc, j), "s")
-            do("Sv%d%d" % (b, hc))
-
-        def k(b, hc, engine):
+        def k_rot(b, hc, add):
             for jp in range(2):
-                s = "%d%d%d" % (b, hc, jp)
-                do("r" + s)
-                do("n" + s)
-                do("nc" + s, "s")
-                do("m1" + s)
-                do("m2" + s)
-            for s in range(2):
-                do("a%d%d%d" % (s, b, hc), engine)
-            do("Sk%d%d" % (b, hc))
+                r_matmul(b, hc, jp)
+                rotate(b, hc, jp)
+            k_add(b, hc, add)
 
-        for label in ("kv0", "x0", "kv1", "x1", "x2", "x3", "v0", "v1", "r0", "r1", "n0", "r2", "r3"):
-            do("L" + label)
-            if label == "v0":
-                load_tables()
-        do("WUkv0", "v")
-        do("WUkv1", "s")
-        do("WQkv0")
-        do("WQkv1")
-        for i in range(2):
-            for h in range(2):
-                do("T%d%d" % (i, h))
-                do("xc%d%d" % (i, h), "sv"[h])
-        do("XQ0")
-        do("WUkv2", "v")
-        do("WUkv3", "v")
-        do("XQ1")
-        do("WQkv2")
-        do("WQkv3")
-        for i in range(2, 4):
-            for h in range(2):
-                do("T%d%d" % (i, h))
-                do("xc%d%d" % (i, h), "s")
-            do("XQ%d" % i)
+        def k_nope(b, hc):
+            for jp in range(2):
+                n_part(b, hc, jp)
+
+        def k_store(b, hc):
+            store(out_0, "k%d%d" % (b, hc), b, hc)
+
+        def k(b, hc, add):
+            for jp in range(2):
+                r_matmul(b, hc, jp)
+                rotate(b, hc, jp)
+                n_part(b, hc, jp)
+            k_add(b, hc, add)
+            k_store(b, hc)
+
+        load_kv(0, 2)
+        load_x(0)
+        load_kv(1)
+        load_x(1)
+        load_v()
+        load_x(2)
+        load_x(3)
+        for g in range(4):
+            load_r(g)
+        load_n()
+        load_tables()
+
+        w_copy("v", "kv0")
+        w_copy("s", "kv1")
+        quantise("kv0", "kv1")
+        x_in(0)
+        quantise("x0")
+        x_in(1)
+        w_copy("s", "kv3")
+        w_copy("v", "kv2")
+        quantise("kv2", "x1", "kv3")
+        for i in (2, 3):
+            x_in(i)
+            quantise("x%d" % i)
         for i in range(4):
-            do("LT%d" % i)
-            for h in range(2):
-                do("T%d%d" % (4 + i, h))
-                do("xc%d%d" % (4 + i, h), "s")
-            do("lc%d" % i, "s")
-            if i < 2:
-                do("WUv%d" % i, "v")
-            else:
-                do("WQv%d" % (i - 2))
-            do("XQ%d" % (4 + i))
-        do("LQ0")
-        do("WUv2", "v")
-        do("LT4")
-        do("lc4", "s")
-        do("LT5")
-        do("lc5", "s")
-        do("LT6")
-        do("lc6", "s")
+            latent(i)
+        w_copy("v", "v0", "v1")
+        x_in(4)
+        quantise("v0", "l0", "v1")
+        x_in(5)
+        quantise("x4")
+        x_in(6)
+        w_copy("v", "v2")
+        quantise("x5", "x6")
+        x_in(7)
+        w_copy("v", "v3")
+        quantise("v2", "x7", "v3")
         v(0, 0)
-        do("LT7")
-        do("lc7", "s")
-        do("WQv2")
+        for i in range(4, 8):
+            latent(i)
+        w_copy("v", "r00", "r10")
         v(0, 1)
-        do("WUr00", "v")
-        do("WUv3", "v")
-        do("LQ1")
-        prep_tables()
-        do("WQr00")
-        w(("r10",))
-        do("WUn0", "s")
+        quantise("l1", "r00", "r10")
+        w_copy("v", "r20", "r30")
+        quantise("r20", "r30")
+        w_copy("v", "n0")
         v(1, 0)
-        w(("r20", "r30"))
-        do("WQv3")
+        quantise("n0")
+        w_copy("v", "r11")
         v(1, 1)
+        prep_tables()
+        k_rot(0, 0, "v")
+        w_copy("s", "r01")
         v(0, 2)
-        do("WQn0")
+        k_nope(0, 0)
+        k_store(0, 0)
+        w_copy("v", "r31")
+        quantise("r11", "r01")
+        w_copy("s", "r21")
         v(1, 2)
-        w(("r01",))
-        k(0, 0, "g")
+        w_copy("v", "n1")
+        quantise("r31", "n1", "r21")
+        k_rot(1, 0, "g")
         v(0, 3)
-        w(("r11",))
-        do("WUr21", "s")
-        k(1, 0, "g")
-        do("WUn1", "s")
-        v(1, 3)
-        w(("r31",))
-        do("WQr21")
+        k_nope(1, 0)
+        k_store(1, 0)
         k(0, 1, "g")
-        k(1, 1, "g")
-        do("WQn1")
-        for hc in range(2, 4):
+        k_rot(1, 1, "g")
+        v(1, 3)
+        k_nope(1, 1)
+        k_store(1, 1)
+        for hc in (2, 3):
             for b in range(2):
-                k(b, hc, "v" if hc == 3 else "g")
-        assert len(set(emitted)) == len(emitted) == len(ops), set(ops) - set(emitted)
+                k(b, hc, "g" if hc == 2 or b == 0 else "v")

@@ -221,9 +221,12 @@ def tile_multiheadlatentattention_pb_kernel(
                     op=ADD,
                 )
 
-        def k_rot(b, hc, add):
+        def k_r(b, hc):
             for jp in range(2):
                 r_matmul(b, hc, jp)
+
+        def k_rot(b, hc, add):
+            for jp in range(2):
                 rotate(b, hc, jp)
             k_add(b, hc, add)
 
@@ -236,7 +239,6 @@ def tile_multiheadlatentattention_pb_kernel(
 
         def k(b, hc, add):
             for jp in range(2):
-                r_matmul(b, hc, jp)
                 rotate(b, hc, jp)
                 n_part(b, hc, jp)
             k_add(b, hc, add)
@@ -275,10 +277,11 @@ def tile_multiheadlatentattention_pb_kernel(
         quantise("x4")
         x_in(6)
         w_copy("v", "v2")
-        quantise("x5", "x6")
+        quantise("x5", "v2", "x6")
         x_in(7)
+        quantise("x7")
         w_copy("v", "v3")
-        quantise("v2", "x7", "v3")
+        quantise("v3")
         v(0, 0)
         for i in range(4, 8):
             latent(i)
@@ -289,30 +292,34 @@ def tile_multiheadlatentattention_pb_kernel(
         quantise("r20", "r30")
         w_copy("v", "n0")
         v(1, 0)
-        quantise("n0")
-        w_copy("v", "r11")
         v(1, 1)
-        prep_tables()
-        k_rot(0, 0, "v")
-        w_copy("s", "r01")
+        w_copy("v", "r11")
+        quantise("n0")
+        w_copy("v", "r31")
         v(0, 2)
+        v(1, 2)
+        k_r(0, 0)
+        w_copy("s", "r01")
+        quantise("r11", "r31")
+        w_copy("v", "r21", "n1")
+        v(0, 3)
+        quantise("r21", "n1", "r01")
+        prep_tables()
+        k_r(1, 0)
+        k_rot(0, 0, "g")
+        v(1, 3)
         k_nope(0, 0)
         k_store(0, 0)
-        w_copy("v", "r31")
-        quantise("r11", "r01")
-        w_copy("s", "r21")
-        v(1, 2)
-        w_copy("v", "n1")
-        quantise("r31", "n1", "r21")
-        k_rot(1, 0, "g")
-        v(0, 3)
-        k_nope(1, 0)
-        k_store(1, 0)
+        k_r(0, 1)
+        k(1, 0, "g")
+        k_r(1, 1)
         k(0, 1, "g")
-        k_rot(1, 1, "g")
-        v(1, 3)
-        k_nope(1, 1)
-        k_store(1, 1)
-        for hc in (2, 3):
-            for b in range(2):
-                k(b, hc, "g" if hc == 2 or b == 0 else "v")
+        k_r(0, 2)
+        k(1, 1, "g")
+        k_r(1, 2)
+        k(0, 2, "g")
+        k_r(0, 3)
+        k(1, 2, "g")
+        k_r(1, 3)
+        k(0, 3, "v")
+        k(1, 3, "v")

@@ -225,9 +225,12 @@ def tile_multiheadlatentattention_pb_kernel(
             for jp in range(2):
                 r_matmul(b, hc, jp)
 
-        def k_rot(b, hc, add):
+        def k_m(b, hc):
             for jp in range(2):
                 rotate(b, hc, jp)
+
+        def k_rot(b, hc, add):
+            k_m(b, hc)
             k_add(b, hc, add)
 
         def k_nope(b, hc):
@@ -236,6 +239,38 @@ def tile_multiheadlatentattention_pb_kernel(
 
         def k_store(b, hc):
             store(out_0, "k%d%d" % (b, hc), b, hc)
+
+        def k_pair(b, hc, hp):
+            heads = cols(hp, 2)
+            pr = bank("r%d%d_%d" % (b, hc, hp))
+            pn = bank("n%d%d_%d" % (b, hc, hp))
+            for j in range(4):
+                for g in range(4):
+                    mx(pr[:, cols(j, 128)], "x%d" % (4 * b + j), cols(g, 128), "r%d%d" % (g, hc // 2), cols(2 * (hc % 2) + hp, 128), g == 0, g == 3)
+            for j in range(4):
+                mx(pn[:, cols(j, 128)], "l%d" % b, cols(j, 128), "n%d" % (hc // 2), cols(2 * (hc % 2) + hp, 128), True, True)
+            k4 = out_tile("k%d%d" % (b, hc))[:, heads, :, :]
+            t4 = tm_tile(b, hc)[:, heads, :, :]
+            r4 = pr[:].rearrange("p (j h d) -> p j h d", j=4, h=2)
+            for out, table in ((k4[:, :, :, 0:64], cos_b), (t4, sin_sw)):
+                nc.vector.tensor_tensor(
+                    out=out.rearrange("p h j d -> p j h d"),
+                    in0=r4,
+                    in1=table[:].unsqueeze(2).to_broadcast([P, 4, 2, 64]),
+                    op=MULT,
+                )
+            copy("s", k4[:, :, :, 64:128].rearrange("p h j d -> p j h d"), pn[:].rearrange("p (j h d) -> p j h d", j=4, h=2))
+            for s in range(2):
+                nc.vector.tensor_tensor(
+                    out=k4[:, :, :, 32 * s : 32 * s + 32],
+                    in0=k4[:, :, :, 32 * s : 32 * s + 32],
+                    in1=t4[:, :, :, 32 - 32 * s : 64 - 32 * s],
+                    op=ADD,
+                )
+            nc.sync.dma_start(
+                out=out_0[b, 4 * hc + 2 * hp : 4 * hc + 2 * hp + 2].rearrange("h (p j) d -> p h (j d)", j=4),
+                in_=outs["k%d%d" % (b, hc)][:, cols(hp, 1024)].rearrange("p (h f) -> p h f", h=2),
+            )
 
         def k(b, hc, add):
             for jp in range(2):
@@ -268,7 +303,9 @@ def tile_multiheadlatentattention_pb_kernel(
         for i in (2, 3):
             x_in(i)
             quantise("x%d" % i)
-        for i in range(4):
+        latent(0)
+        w_copy("s", "v2")
+        for i in range(1, 4):
             latent(i)
         w_copy("v", "v0", "v1")
         x_in(4)
@@ -276,12 +313,11 @@ def tile_multiheadlatentattention_pb_kernel(
         x_in(5)
         quantise("x4")
         x_in(6)
-        w_copy("v", "v2")
-        quantise("x5", "v2", "x6")
-        x_in(7)
-        quantise("x7")
+        quantise("v2", "x5")
         w_copy("v", "v3")
-        quantise("v3")
+        quantise("x6")
+        x_in(7)
+        quantise("v3", "x7")
         v(0, 0)
         for i in range(4, 8):
             latent(i)
@@ -320,6 +356,6 @@ def tile_multiheadlatentattention_pb_kernel(
         k(0, 2, "g")
         k_r(0, 3)
         k(1, 2, "g")
-        k_r(1, 3)
         k(0, 3, "v")
-        k(1, 3, "v")
+        k_pair(1, 3, 0)
+        k_pair(1, 3, 1)

@@ -319,43 +319,64 @@ def tile_multiheadlatentattention_pb_kernel(
         x_in(7)
         quantise("v3", "x7")
         v(0, 0)
-        for i in range(4, 8):
-            latent(i)
-        w_copy("v", "r00", "r10")
+        latent(4)
+        latent(5)
         v(0, 1)
-        quantise("l1", "r00", "r10")
+        w_copy("v", "r00", "r10")
+        latent(6)
+        latent(7)
+        v(0, 2)
+        quantise("r00", "r10")
         w_copy("v", "r20", "r30")
-        quantise("r20", "r30")
+        quantise("l1", "r20", "r30")
         w_copy("v", "n0")
+        v(0, 3)
         v(1, 0)
-        v(1, 1)
         w_copy("v", "r11")
         quantise("n0")
         w_copy("v", "r31")
-        v(0, 2)
-        v(1, 2)
+        v(1, 1)
         k_r(0, 0)
         w_copy("s", "r01")
         quantise("r11", "r31")
         w_copy("v", "r21", "n1")
-        v(0, 3)
+        v(1, 2)
         quantise("r21", "n1", "r01")
         prep_tables()
         k_r(1, 0)
         k_rot(0, 0, "g")
-        v(1, 3)
-        k_nope(0, 0)
+        v(1, 3, range(0, 2))
+        r_matmul(0, 1, 0)
+        v(1, 3, range(2, 4))
+        n_part(0, 0, 0)
+        r_matmul(0, 1, 1)
+        n_part(0, 0, 1)
         k_store(0, 0)
-        k_r(0, 1)
         k(1, 0, "g")
-        k_r(1, 1)
-        k(0, 1, "g")
-        k_r(0, 2)
-        k(1, 1, "g")
-        k_r(1, 2)
-        k(0, 2, "g")
-        k_r(0, 3)
-        k(1, 2, "g")
+        n_part(0, 1, 0)
+        r_matmul(1, 1, 0)
+        n_part(0, 1, 1)
+        r_matmul(1, 1, 1)
+        k_rot(0, 1, "g")
+        k_store(0, 1)
+        n_part(1, 1, 0)
+        r_matmul(0, 2, 0)
+        n_part(1, 1, 1)
+        r_matmul(0, 2, 1)
+        k_rot(1, 1, "g")
+        k_store(1, 1)
+        n_part(0, 2, 0)
+        r_matmul(1, 2, 0)
+        n_part(0, 2, 1)
+        r_matmul(1, 2, 1)
+        k_rot(0, 2, "g")
+        k_store(0, 2)
+        n_part(1, 2, 0)
+        r_matmul(0, 3, 0)
+        n_part(1, 2, 1)
+        r_matmul(0, 3, 1)
+        k_rot(1, 2, "g")
+        k_store(1, 2)
         k(0, 3, "v")
         k_pair(1, 3, 0)
         k_pair(1, 3, 1)

from contextlib import ExitStack

import concourse.mybir as mybir
from concourse.masks import make_identity

BF16 = mybir.dt.bfloat16
F32 = mybir.dt.float32
U32 = mybir.dt.uint32
U8 = mybir.dt.uint8
FP8X4 = mybir.dt.float8_e4m3fn_x4
MULT = mybir.AluOpType.mult
ADD = mybir.AluOpType.add

P = 128
FLOPS = 2 * 1024 * (2048 * 512 + 2048 * 1024 + 512 * 1024 + 512 * 2048)


def tile_multiheadlatentattention_pb_kernel(
    tc, x, Wkv_d, Wk_nope, Wv_u, Wrk, cos, sin, out_0, out_1
):
    nc = tc.nc
    with ExitStack() as ctx:
        const = ctx.enter_context(tc.tile_pool(name="const", bufs=1))
        big = ctx.enter_context(tc.tile_pool(name="big", bufs=12))
        vraw = ctx.enter_context(tc.tile_pool(name="vraw", bufs=1))
        grp = ctx.enter_context(tc.tile_pool(name="grp", bufs=6))
        keep = ctx.enter_context(tc.tile_pool(name="keep", bufs=1))
        tmpp = ctx.enter_context(tc.tile_pool(name="tmpp", bufs=2))
        psum = ctx.enter_context(tc.psum_pool(name="psum", bufs=8))
        ctx.enter_context(tc.manual_schedule())

        ident = const.tile([P, P], F32, name="ident")
        make_identity(nc, ident[:])
        cos_b = const.tile([P, 4, 64], BF16, name="cos_b")
        sin_b = const.tile([P, 4, 64], BF16, name="sin_b")
        sin_sw = const.tile([P, 4, 64], BF16, name="sin_sw")

        raws = {}
        groups = {}
        quants = {}
        banks = {}
        outs = {}
        tms = {}

        def cols(i, w):
            return slice(i * w, i * w + w)

        def load_x(c, parts=1):
            rows = x[c // 2].rearrange("(p j) k -> p j k", j=4)
            raws["x%d" % c] = big.tile([P, 4096], BF16, tag="big", name="rawx%d" % c)
            dst = raws["x%d" % c][:].rearrange("p (j k) -> p j k", j=2)
            for i in range(parts):
                js = cols(i, 2 // parts)
                nc.sync.dma_start(out=dst[:, js, :], in_=rows[:, 2 * (c % 2) : 2 * (c % 2) + 2, :][:, js, :])

        def load_kv(c, parts=1):
            raws["kv%d" % c] = big.tile([P, 4096], BF16, tag="big", name="rawkv%d" % c)
            src = Wkv_d[1024 * c : 1024 * c + 1024, :].rearrange("(g u p e) n -> p (g u) (e n)", g=2, u=2, p=P, e=2)
            dst = raws["kv%d" % c][:].rearrange("p (a f) -> p a f", a=4)
            for i in range(parts):
                part = cols(i, 4 // parts)
                nc.sync.dma_start(out=dst[:, part, :], in_=src[:, part, :])

        def load_v():
            raws["v"] = vraw.tile([P, 8192], BF16, name="rawv")
            for c in range(2):
                nc.sync.dma_start(
                    out=raws["v"][:, cols(c, 4096)].rearrange("p (t n) -> p t n", t=2),
                    in_=Wv_u.rearrange("(p t) n -> p t n", t=4)[:, cols(c, 2), :],
                )

        def load_n():
            raws["n"] = big.tile([P, 4096], BF16, tag="big", name="rawn")
            nc.sync.dma_start(out=raws["n"][:].rearrange("p (t n) -> p t n", t=4), in_=Wk_nope.rearrange("(p t) n -> p t n", t=4))

        def load_r(g):
            raws["r%d" % g] = big.tile([P, 4096], BF16, tag="big", name="rawr%d" % g)
            nc.sync.dma_start(
                out=raws["r%d" % g][:].rearrange("p (u f) -> p u f", u=2),
                in_=Wrk[512 * g : 512 * g + 512, :].rearrange("(u p e) n -> p u (e n)", u=2, p=P, e=2),
            )

        def load_tables():
            nc.sync.dma_start(out=cos_b[:], in_=cos.rearrange("(p j) d -> p j d", j=4))
            nc.sync.dma_start(out=sin_b[:], in_=sin.rearrange("(p j) d -> p j d", j=4))

        def prep_tables():
            nc.vector.tensor_copy(out=sin_sw[:, :, 0:32], in_=sin_b[:, :, 32:64])
            nc.vector.tensor_scalar_mul(out=sin_sw[:, :, 32:64], in0=sin_b[:, :, 0:32], scalar1=-1.0)

        def copy(engine, out, in_):
            if engine == "v":
                nc.vector.tensor_copy(out=out, in_=in_)
            else:
                nc.scalar.copy(out=out, in_=in_)

        def bank(key):
            banks[key] = psum.tile([P, 512], F32, tag="ps", name="ps" + key)
            return banks[key]

        def group(key):
            if key not in groups:
                groups[key] = grp.tile([P, 2048], BF16, tag="g", name="g" + key, align_bytes=64)
            return groups[key]

        def quantise(*keys):
            for key in keys:
                codes = keep.tile([P, 512], U32, name="c_" + key, align_bytes=64)
                scales = keep.tile([P, 512], U8, name="s_" + key, align_bytes=64)
                nc.vector.quantize_mx(out=codes[:].bitcast(FP8X4), scales=scales[:], in_=groups[key][:])
                quants[key] = (codes, scales)

        def mx(out, a, acols, b, bcols, start, stop):
            qa = quants[a]
            qb = quants[b]
            nc.tensor.matmul_mx(
                out=out,
                lhsT=qa[0][:, acols].bitcast(FP8X4),
                lhsT_scale=qa[1][:, acols],
                rhs=qb[0][:, bcols].bitcast(FP8X4),
                rhs_scale=qb[1][:, bcols],
                start=start,
                stop=stop,
            )

        def x_in(i, engines="ss"):
            xw = raws["x%d" % (i // 2)][:].bitcast(F32)
            gw = group("x%d" % i)[:].bitcast(F32).rearrange("p (g r u) -> p g r u", g=4, u=2)
            for h in range(2):
                xt = bank("x%d%d" % (i, h))
                xt3 = xt[:].rearrange("p (a r) -> p a r", a=4)
                for a in range(4):
                    c0 = 1024 * (i % 2) + 512 * h + 128 * a
                    nc.tensor.transpose(xt3[:, a, :], xw[:, c0 : c0 + 128], ident[:])
                copy(engines[h], gw[:, 2 * h : 2 * h + 2, :, :], xt[:].rearrange("p (g u r) -> p g r u", g=2, u=2))

        def w_copy(engine, *labels):
            for label in labels:
                kind = label[: len(label) - 1]
                i = int(label[len(label) - 1])
                dst = group(label)[:]
                if kind == "kv":
                    src = raws["kv%d" % (i // 2)][:].rearrange("p (g t n) -> p g t n", g=2, t=4)[:, i % 2, :, :]
                    copy(engine, dst.rearrange("p (t m j) -> p t m j", t=4, j=4), src.rearrange("p j (m t) -> p t m j", t=4))
                else:
                    src = raws[kind][:].rearrange("p (t n) -> p t n", t=4)[:, :, cols(i, 512)]
                    copy(engine, dst.rearrange("p (c i t) -> p c t i", i=4, t=4), src.rearrange("p t (c i) -> p c t i", i=4))

        def latent(i, engine="s"):
            pl = bank("l%d" % i)
            pl3 = pl[:].rearrange("p (t r) -> p t r", t=4)
            for t in range(4):
                for g in range(4):
                    mx(pl3[:, t, :], "kv%d" % g, cols(t, 128), "x%d" % i, cols(g, 128), g == 0, g == 3)
            g4 = group("l%d" % (i // 4))[:].rearrange("p (j r t) -> p j r t", j=4, t=4)
            copy(engine, g4[:, i % 4, :, :], pl[:].rearrange("p (t r) -> p r t", t=4))

        def out_tile(key):
            if key not in outs:
                outs[key] = big.tile([P, 2048], F32, tag="big", name="o" + key)
            return outs[key][:].rearrange("p (h j d) -> p h j d", h=4, j=4)

        def store(dram, key, b, hc):
            nc.sync.dma_start(
                out=dram[b, 4 * hc : 4 * hc + 4].rearrange("h (p j) d -> p h (j d)", j=4),
                in_=outs[key][:].rearrange("p (h f) -> p h f", h=4),
            )

        def v(b, hc, js=range(4)):
            key = "v%d%d" % (b, hc)
            for j in js:
                pv = bank("%s%d" % (key, j))
                mx(pv[:], "l%d" % b, cols(j, 128), "v%d" % hc, cols(0, 512), True, True)
                copy("s", out_tile(key)[:, :, j, :], pv[:].rearrange("p (h d) -> p h d", h=4))
            if 3 in js:
                store(out_1, key, b, hc)

        def r_matmul(b, hc, jp):
            pr3 = bank("r%d%d%d" % (b, hc, jp))[:].rearrange("p (j n) -> p j n", j=2)
            for jj in range(2):
                for g in range(4):
                    mx(pr3[:, jj, :], "x%d" % (4 * b + 2 * jp + jj), cols(g, 128), "r%d%d" % (g, hc // 2), cols(hc % 2, 256), g == 0, g == 3)

        def n_part(b, hc, jp):
            pn = bank("n%d%d%d" % (b, hc, jp))
            pn3 = pn[:].rearrange("p (j n) -> p j n", j=2)
            for jj in range(2):
                mx(pn3[:, jj, :], "l%d" % b, cols(2 * jp + jj, 128), "n%d" % (hc // 2), cols(hc % 2, 256), True, True)
            copy(
                "s",
                out_tile("k%d%d" % (b, hc))[:, :, cols(jp, 2), 64:128].rearrange("p h j d -> p j h d"),
                pn[:].rearrange("p (j h d) -> p j h d", j=2, h=4),
            )

        def tm_tile(b, hc):
            key = "t%d%d" % (b, hc)
            if key not in tms:
                tms[key] = tmpp.tile([P, 1024], F32, tag="tmp", name=key)
            return tms[key][:].rearrange("p (h j d) -> p h j d", h=4, j=4)

        def rotate(b, hc, jp):
            js = cols(jp, 2)
            r4 = banks["r%d%d%d" % (b, hc, jp)][:].rearrange("p (j h d) -> p j h d", j=2, h=4)
            k4 = out_tile("k%d%d" % (b, hc))
            for out, table in ((k4[:, :, js, 0:64], cos_b), (tm_tile(b, hc)[:, :, js, :], sin_sw)):
                nc.vector.tensor_tensor(
                    out=out.rearrange("p h j d -> p j h d"),
                    in0=r4,
                    in1=table[:, js, :].unsqueeze(2).to_broadcast([P, 2, 4, 64]),
                    op=MULT,
                )

        def k_add(b, hc, engine):
            k4 = out_tile("k%d%d" % (b, hc))
            t4 = tm_tile(b, hc)
            for s in range(2):
                (nc.gpsimd if engine == "g" else nc.vector).tensor_tensor(
                    out=k4[:, :, :, 32 * s : 32 * s + 32],
                    in0=k4[:, :, :, 32 * s : 32 * s + 32],
                    in1=t4[:, :, :, 32 - 32 * s : 64 - 32 * s],
                    op=ADD,
                )

        def k_r(b, hc):
            for jp in range(2):
                r_matmul(b, hc, jp)

        def k_m(b, hc):
            for jp in range(2):
                rotate(b, hc, jp)

        def k_rot(b, hc, add):
            k_m(b, hc)
            k_add(b, hc, add)

        def k_nope(b, hc):
            for jp in range(2):
                n_part(b, hc, jp)

        def k_store(b, hc):
            store(out_0, "k%d%d" % (b, hc), b, hc)

        def k_pair(b, hc, hp):
            heads = cols(hp, 2)
            pr = bank("r%d%d_%d" % (b, hc, hp))
            pn = bank("n%d%d_%d" % (b, hc, hp))
            for j in range(4):
                for g in range(4):
                    mx(pr[:, cols(j, 128)], "x%d" % (4 * b + j), cols(g, 128), "r%d%d" % (g, hc // 2), cols(2 * (hc % 2) + hp, 128), g == 0, g == 3)
            for j in range(4):
                mx(pn[:, cols(j, 128)], "l%d" % b, cols(j, 128), "n%d" % (hc // 2), cols(2 * (hc % 2) + hp, 128), True, True)
            k4 = out_tile("k%d%d" % (b, hc))[:, heads, :, :]
            t4 = tm_tile(b, hc)[:, heads, :, :]
            r4 = pr[:].rearrange("p (j h d) -> p j h d", j=4, h=2)
            for out, table in ((k4[:, :, :, 0:64], cos_b), (t4, sin_sw)):
                nc.vector.tensor_tensor(
                    out=out.rearrange("p h j d -> p j h d"),
                    in0=r4,
                    in1=table[:].unsqueeze(2).to_broadcast([P, 4, 2, 64]),
                    op=MULT,
                )
            copy("s", k4[:, :, :, 64:128].rearrange("p h j d -> p j h d"), pn[:].rearrange("p (j h d) -> p j h d", j=4, h=2))
            for s in range(2):
                nc.vector.tensor_tensor(
                    out=k4[:, :, :, 32 * s : 32 * s + 32],
                    in0=k4[:, :, :, 32 * s : 32 * s + 32],
                    in1=t4[:, :, :, 32 - 32 * s : 64 - 32 * s],
                    op=ADD,
                )
            nc.sync.dma_start(
                out=out_0[b, 4 * hc + 2 * hp : 4 * hc + 2 * hp + 2].rearrange("h (p j) d -> p h (j d)", j=4),
                in_=outs["k%d%d" % (b, hc)][:, cols(hp, 1024)].rearrange("p (h f) -> p h f", h=2),
            )

        def k(b, hc, add):
            for jp in range(2):
                rotate(b, hc, jp)
                n_part(b, hc, jp)
            k_add(b, hc, add)
            k_store(b, hc)

        load_kv(0, 2)
        load_x(0)
        load_kv(1)
        load_x(1)
        load_v()
        load_x(2)
        load_x(3)
        for g in range(4):
            load_r(g)
        load_n()
        load_tables()

        w_copy("v", "kv0")
        w_copy("s", "kv1")
        quantise("kv0", "kv1")
        x_in(0)
        quantise("x0")
        x_in(1)
        w_copy("s", "kv3")
        w_copy("v", "kv2")
        quantise("kv2", "x1", "kv3")
        for i in (2, 3):
            x_in(i)
            quantise("x%d" % i)
        latent(0)
        w_copy("s", "v2")
        for i in range(1, 4):
            latent(i)
        w_copy("v", "v0", "v1")
        x_in(4)
        quantise("v0", "l0", "v1")
        x_in(5)
        quantise("x4")
        x_in(6)
        quantise("v2", "x5")
        w_copy("v", "v3")
        quantise("x6")
        x_in(7)
        quantise("v3", "x7")
        v(0, 0)
        latent(4)
        latent(5)
        v(0, 1)
        w_copy("v", "r00", "r10")
        latent(6)
        latent(7)
        v(0, 2)
        quantise("r00", "r10")
        w_copy("v", "r20", "r30")
        quantise("l1", "r20", "r30")
        w_copy("v", "n0")
        v(0, 3)
        v(1, 0)
        w_copy("v", "r11")
        quantise("n0")
        w_copy("v", "r31")
        v(1, 1)
        k_r(0, 0)
        w_copy("s", "r01")
        quantise("r11", "r31")
        w_copy("v", "r21", "n1")
        v(1, 2)
        quantise("r21", "n1", "r01")
        prep_tables()
        k_r(1, 0)
        k_rot(0, 0, "g")
        v(1, 3, range(0, 2))
        r_matmul(0, 1, 0)
        v(1, 3, range(2, 4))
        n_part(0, 0, 0)
        r_matmul(0, 1, 1)
        n_part(0, 0, 1)
        k_store(0, 0)
        k(1, 0, "g")
        n_part(0, 1, 0)
        r_matmul(1, 1, 0)
        n_part(0, 1, 1)
        r_matmul(1, 1, 1)
        k_rot(0, 1, "g")
        k_store(0, 1)
        n_part(1, 1, 0)
        r_matmul(0, 2, 0)
        n_part(1, 1, 1)
        r_matmul(0, 2, 1)
        k_rot(1, 1, "g")
        k_store(1, 1)
        n_part(0, 2, 0)
        r_matmul(1, 2, 0)
        n_part(0, 2, 1)
        r_matmul(1, 2, 1)
        k_rot(0, 2, "g")
        k_store(0, 2)
        n_part(1, 2, 0)
        r_matmul(0, 3, 0)
        n_part(1, 2, 1)
        r_matmul(0, 3, 1)
        k_rot(1, 2, "g")
        k_store(1, 2)
        k(0, 3, "v")
        k_pair(1, 3, 0)
        k_pair(1, 3, 1)
